import numpy as np
import ml_dtypes


def mxq(x, axis, fmt="e4m3"):
    dtype, down = {"e4m3": (ml_dtypes.float8_e4m3fn, 7), "e5m2": (ml_dtypes.float8_e5m2, 14)}[fmt]
    v = np.moveaxis(np.asarray(x, np.float32).astype(ml_dtypes.bfloat16).astype(np.float64), axis, -1)
    blocks = v.reshape(v.shape[:-1] + (-1, 32))
    amax = np.abs(blocks).max(-1, keepdims=True)
    byte = np.maximum(np.where(amax > 0, np.frexp(amax)[1] - 1 + 127, 0) - down, 1)
    scale = np.exp2(byte - 127.0)
    codes = (blocks / scale).astype(np.float32).astype(dtype).astype(np.float64)
    return np.moveaxis((codes * scale).reshape(v.shape), -1, axis)


WIDE = False


def mx_kscale(k):
    if not WIDE:
        return np.ones(k)
    levels = np.array([10, -10, 5, -5, 0])
    a = np.random.permutation(np.resize(levels, k // 512 * 4)).reshape(k // 512, 4)
    idx = np.arange(k)
    return np.exp2(a[idx // 512, idx % 128 // 32])


BF16 = ml_dtypes.bfloat16


def bf(x):
    return np.asarray(x, np.float32).astype(BF16)


def f64(x):
    return np.asarray(x).astype(np.float64)


B, HD, NH, H, W, F = 2, 512, 8, 32, 64, 1024


def rms_in(x, w, eps=1e-8):
    std = np.std(x, axis=(-2, -1), keepdims=True, ddof=1)
    return x / (std + eps) * w[None, :, None, None]


def erf(v):
    u = np.clip(v, -6.0, 6.0)
    u2 = 2.0 * u * u
    term = u.copy()
    tot = u.copy()
    for n in range(1, 120):
        term = term * u2 / (2 * n + 1)
        tot = tot + term
    return 2.0 / np.sqrt(np.pi) * np.exp(-u * u) * tot


def gelu(v):
    return 0.5 * v * (1.0 + erf(v / np.sqrt(2.0)))


def setup_inputs():
    n = np.random.standard_normal
    s = mx_kscale(HD)
    return {"x2": bf((1.2 * n((B, HD, H, W)) + 1.2 * n((B, HD, 1, 1))) * s[None, :, None, None]),
            "fc1_w": bf(n((F, HD)) * 0.6 / np.sqrt(HD) / s[None, :]),
            "fc1_b": bf(0.2 * n(F)),
            "fc2_w": bf(n((HD, F)) / np.sqrt(F)),
            "fc2_b": bf(0.1 * n(HD)),
            "mlp_norm_w": bf(1.0 + 0.1 * n(HD)),
            "gamma_mlp": bf((0.5 + 0.2 * n(HD)) * s)}


def reference(x2, fc1_w, fc1_b, fc2_w, fc2_b, mlp_norm_w, gamma_mlp):
    x2 = f64(x2)
    xt = x2.transpose(0, 2, 3, 1)
    h = gelu((mxq(xt, 3, "e4m3") @ mxq(f64(fc1_w), 1, "e4m3").T) + f64(fc1_b))
    m = (mxq(h, 3, "e4m3") @ mxq(f64(fc2_w), 1, "e4m3").T) + f64(fc2_b)
    m = m.transpose(0, 3, 1, 2)
    m = rms_in(m, f64(mlp_norm_w))
    return x2 + f64(gamma_mlp)[None, :, None, None] * m

@@ -1,0 +1,281 @@
+from contextlib import ExitStack
+
+import concourse.bass as bass
+import concourse.mybir as mybir
+import concourse.tile as tile
+from concourse.masks import make_identity
+
+F32 = mybir.dt.float32
+BF16 = mybir.dt.bfloat16
+U32 = mybir.dt.uint32
+U8 = mybir.dt.uint8
+FP8X4 = mybir.dt.float8_e4m3fn_x4
+ACT = mybir.ActivationFunctionType
+ALU = mybir.AluOpType
+
+FLOPS = 2 * 4096 * 512 * 1024 * 2
+
+P = 128
+NPOS = 2048
+NT = 512
+NB = 2
+
+X_ENG = {}
+H_ENG = {(1, 0, 0): "s", (1, 0, 1): "s", (1, 1, 0): "s", (1, 1, 1): "s",
+         (1, 2, 0): "s", (1, 2, 1): "s", (1, 3, 0): "s", (1, 3, 1): "s"}
+HX_ENG = {0: "g", 1: "s"}
+
+
+def regroup(nc, eng, dst, src):
+    d = dst.rearrange("p (c i) t -> p c t i", i=4)
+    s = src.rearrange("p t (c i) -> p c t i", i=4)
+    if eng == "v":
+        nc.vector.tensor_copy(out=d, in_=s)
+    elif eng == "s":
+        nc.scalar.copy(out=d, in_=s)
+    else:
+        nc.gpsimd.tensor_scalar(out=d, in0=s, scalar1=1.0, scalar2=0.0, op0=ALU.mult, op1=ALU.add)
+
+
+def tile_axialattentionblock_pc_t_kernel(tc, x2, fc1_w, fc1_b, fc2_w, fc2_b, mlp_norm_w, gamma_mlp, out):
+    nc = tc.nc
+    with ExitStack() as ctx:
+        const = ctx.enter_context(tc.tile_pool(name="const", bufs=1))
+        xgp = ctx.enter_context(tc.tile_pool(name="xgp", bufs=3))
+        hsp = ctx.enter_context(tc.tile_pool(name="hsp", bufs=4))
+        hgp = ctx.enter_context(tc.tile_pool(name="hgp", bufs=4))
+        xbp = ctx.enter_context(tc.tile_pool(name="xbp", bufs=8))
+        otp = ctx.enter_context(tc.tile_pool(name="otp", bufs=3))
+        sml = ctx.enter_context(tc.tile_pool(name="sml", bufs=3))
+        psa = ctx.enter_context(tc.psum_pool(name="psa", bufs=2))
+        psb = ctx.enter_context(tc.psum_pool(name="psb", bufs=6))
+
+        xv = x2.rearrange("b (u q e) h w -> q b u e (h w)", u=2, q=P, e=2)
+        ov = out.rearrange("b (u q e) h w -> q b u e (h w)", u=2, q=P, e=2)
+
+        zero1 = const.tile([P, 1], F32)
+        nc.vector.memset(zero1[:], 0.0)
+        warm = const.tile([P, 1], F32)
+        nc.scalar.activation(out=warm[:], in_=zero1[:], func=ACT.Gelu)
+        half = const.tile([P, 1], F32)
+        nc.vector.memset(half[:], 0.5)
+        ident = const.tile([P, P], F32)
+        make_identity(nc, ident[:])
+        vecs = const.tile([P, 256], BF16)
+        nc.vector.memset(vecs[:], 0.0)
+
+        xs = [const.tile([P, 4, NPOS], BF16, name="xs%d" % b) for b in range(NB)]
+        w1raw = const.tile([P, 8, 512], BF16)
+        w2raw = const.tile([P, 4, 1024], BF16)
+        nc.scalar.dma_start(out=vecs[0:4, :], in_=fc1_b.rearrange("(r k) -> r k", r=4))
+        nc.scalar.dma_start(out=vecs[4:6, :], in_=fc2_b.rearrange("(r k) -> r k", r=2))
+        nc.scalar.dma_start(out=vecs[6:8, :], in_=mlp_norm_w.rearrange("(r k) -> r k", r=2))
+        nc.scalar.dma_start(out=vecs[8:10, :], in_=gamma_mlp.rearrange("(r k) -> r k", r=2))
+
+        def load_x(b, c0, c1):
+            for u in range(2):
+                nc.sync.dma_start(out=xs[b][:, 2 * u:2 * u + 2, c0:c1], in_=xv[:, b, u, :, c0:c1])
+
+        w1d = fc1_w.rearrange("(r m e) c -> m r (e c)", r=4, m=P, e=2)
+        w1r = w1raw[:].rearrange("m (r e) c -> m r (e c)", e=2)
+        load_x(0, 0, NT)
+        nc.sync.dma_start(out=w1r[:, 0:2, :], in_=w1d[:, 0:2, :])
+        nc.sync.dma_start(out=w1r[:, 2:4, :], in_=w1d[:, 2:4, :])
+        for n in range(1, 4):
+            load_x(0, n * NT, (n + 1) * NT)
+        nc.sync.dma_start(out=w2raw[:].rearrange("m (u e) f -> m u (e f)", e=2),
+                          in_=fc2_w.rearrange("(u m e) f -> m u (e f)", u=2, m=P, e=2))
+        load_x(1, 0, NPOS)
+
+        pt = psa.tile([P, P], F32, tag="p1")
+        nc.tensor.transpose(pt[:], vecs[:].bitcast(F32), ident[:])
+        prw = const.tile([P, 16], F32)
+        nc.vector.tensor_copy(out=prw[:, 0:10], in_=pt[:, 0:10])
+        prm = const.tile([P, 20], F32)
+        nc.vector.tensor_copy(out=prm[:], in_=prw[:, 0:10].bitcast(BF16))
+        gwb = const.tile([P, 4, 2], F32)
+        nc.vector.tensor_tensor(out=gwb[:, :, 0], in0=prm[:, 12:16], in1=prm[:, 16:20], op=ALU.mult)
+        nc.vector.tensor_tensor(out=gwb[:, :, 1], in0=gwb[:, :, 0], in1=prm[:, 8:12], op=ALU.mult)
+
+        w1g = const.tile([P, 4096], BF16, align_bytes=64)
+        w1c = const.tile([P, 1024], U32, align_bytes=64)
+        w1s = const.tile([P, 1024], U8, align_bytes=64)
+        w1g32 = w1g[:].bitcast(F32).rearrange("q (j m u) -> q j m u", j=8, m=P, u=2)
+        for jp in range(4):
+            wt = psa.tile([P, 2, 2, P], F32, tag="p1", name="wt1") if jp % 2 == 0 else psb.tile([P, 2, 2, P], F32, tag="m2", name="wt1b")
+            for jj in range(2):
+                wsrc = w1raw[:, 2 * jp + jj, :].bitcast(F32)
+                for u in range(2):
+                    nc.tensor.transpose(wt[:, jj, u, :], wsrc[:, P * u:P * u + P], ident[:])
+            src = wt[:].rearrange("q j u m -> q j m u")
+            if jp % 2 == 0:
+                nc.vector.tensor_copy(out=w1g32[:, 2 * jp:2 * jp + 2, :, :], in_=src)
+            else:
+                nc.scalar.copy(out=w1g32[:, 2 * jp:2 * jp + 2, :, :], in_=src)
+            if jp % 2 == 1:
+                h0 = (jp // 2) * 512
+                nc.vector.quantize_mx(out=w1c[:, h0:h0 + 512].bitcast(FP8X4), scales=w1s[:, h0:h0 + 512],
+                                      in_=w1g[:, 4 * h0:4 * h0 + 2048])
+
+        xc = const.tile([P, 8, NT], U32, align_bytes=64)
+        xsc = const.tile([P, 8, NT], U8, align_bytes=64)
+        hc = const.tile([P, 16, NT], U32, align_bytes=64)
+        hsc = const.tile([P, 16, NT], U8, align_bytes=64)
+
+        def x_prep(b, n):
+            xg = xgp.tile([P, NT, 4], BF16, align_bytes=64)
+            regroup(nc, X_ENG.get((b, n), "v"), xg[:], xs[b][:, :, n * NT:(n + 1) * NT])
+            k = b * 4 + n
+            nc.vector.quantize_mx(out=xc[:, k, :].bitcast(FP8X4), scales=xsc[:, k, :],
+                                  in_=xg[:].rearrange("p w t -> p (w t)"))
+
+        def mm1(b, n, g):
+            k = b * 4 + n
+            hs = hsp.tile([P, 4, NT], BF16)
+            for t in range(4):
+                j = 4 * g + t
+                p1 = psa.tile([P, NT], F32, tag="p1")
+                nc.tensor.matmul_mx(out=p1[:], lhsT=w1c[:, P * j:P * j + P].bitcast(FP8X4),
+                                    lhsT_scale=w1s[:, P * j:P * j + P],
+                                    rhs=xc[:, k, :].bitcast(FP8X4), rhs_scale=xsc[:, k, :],
+                                    start=True, stop=True)
+                nc.scalar.activation(out=hs[:, t, :], in_=p1[:], func=ACT.Gelu, bias=prm[:, j:j + 1], scale=1.0)
+            state[(b, n, g, "hs")] = hs
+
+        def h_regroup(b, n, g):
+            hg = hgp.tile([P, NT, 4], BF16, align_bytes=64)
+            regroup(nc, H_ENG.get((b, n, g), "v"), hg[:], state[(b, n, g, "hs")][:])
+            state[(b, n, g, "hg")] = hg
+
+        def h_quant(b, n, g):
+            k = b * 4 + n
+            nc.vector.quantize_mx(out=hc[:, 2 * k + g, :].bitcast(FP8X4), scales=hsc[:, 2 * k + g, :],
+                                  in_=state[(b, n, g, "hg")][:].rearrange("p w t -> p (w t)"))
+
+        w2g = const.tile([P, 4096], BF16, align_bytes=64)
+        w2c = const.tile([P, 2, 512], U32, align_bytes=64)
+        w2s = const.tile([P, 2, 512], U8, align_bytes=64)
+
+        def w2_prep():
+            w2g32 = w2g[:].bitcast(F32).rearrange("q (g i m u) -> q g i m u", g=2, i=4, m=P, u=2)
+            for i in range(4):
+                wt = psb.tile([P, 4, P], F32, tag="m2", name="wt2")
+                wsrc = w2raw[:, i, :].bitcast(F32)
+                for r in range(4):
+                    nc.tensor.transpose(wt[:, r, :], wsrc[:, P * r:P * r + P], ident[:])
+                src = wt[:].rearrange("q (g u) m -> q g m u", g=2)
+                if i % 2 == 0:
+                    nc.vector.tensor_copy(out=w2g32[:, :, i, :, :], in_=src)
+                else:
+                    nc.scalar.copy(out=w2g32[:, :, i, :, :], in_=src)
+            for g in range(2):
+                nc.vector.quantize_mx(out=w2c[:, g, :].bitcast(FP8X4), scales=w2s[:, g, :],
+                                      in_=w2g[:, 2048 * g:2048 * g + 2048])
+
+        state = {}
+
+        def unit_a(b, i):
+            banks = []
+            for n in range(4):
+                k = b * 4 + n
+                m2 = psb.tile([P, NT], F32, tag="m2", name="m2")
+                for g in range(2):
+                    nc.tensor.matmul_mx(out=m2[:], lhsT=w2c[:, g, P * i:P * i + P].bitcast(FP8X4),
+                                        lhsT_scale=w2s[:, g, P * i:P * i + P],
+                                        rhs=hc[:, 2 * k + g, :].bitcast(FP8X4), rhs_scale=hsc[:, 2 * k + g, :],
+                                        start=(g == 0), stop=(g == 1))
+                banks.append(m2)
+            state[(b, i, "banks")] = banks
+
+        def unit_b(b, i):
+            banks = state[(b, i, "banks")]
+            st = sml.tile([P, 4, 6], F32)
+            for n in range(4):
+                nc.vector.bn_stats(out=st[:, n, :], in_=banks[n][:])
+            mv = sml.tile([P, 2], F32)
+            nc.vector.bn_aggr(out=mv[:], in_=st[:].rearrange("p n s -> p (n s)"))
+            sd = sml.tile([P, 1], F32)
+            nc.gpsimd.tensor_tensor(out=sd[:], in0=mv[:, 1:2], in1=half[:], op=ALU.pow)
+            state[(b, i, "sd")] = sd
+
+        def unit_c1(b, i):
+            sd = state[(b, i, "sd")]
+            se = sml.tile([P, 1], F32)
+            nc.vector.tensor_scalar(out=se[:], in0=sd[:], scalar1=(NPOS / (NPOS - 1.0)) ** 0.5, scalar2=1e-8,
+                                    op0=ALU.mult, op1=ALU.add)
+            rc = sml.tile([P, 1], F32)
+            nc.vector.reciprocal(out=rc[:], in_=se[:])
+            ab = sml.tile([P, 2], F32)
+            nc.vector.tensor_scalar(out=ab[:], in0=gwb[:, i, :], scalar1=rc[:, 0:1], scalar2=None, op0=ALU.mult)
+            xbs = []
+            for n in range(4):
+                cs = slice(n * NT, (n + 1) * NT)
+                xb = xbp.tile([P, NT], F32, name="xb")
+                if HX_ENG[b] == "g":
+                    nc.gpsimd.tensor_scalar(out=xb[:], in0=xs[b][:, i, cs], scalar1=1.0, scalar2=ab[:, 1:2],
+                                            op0=ALU.mult, op1=ALU.add)
+                else:
+                    nc.scalar.activation(out=xb[:], in_=xs[b][:, i, cs], func=ACT.Identity, bias=ab[:, 1:2], scale=1.0)
+                xbs.append(xb)
+            state[(b, i, "ab")] = ab
+            state[(b, i, "xbs")] = xbs
+
+        def unit_c2(b, i):
+            banks = state[(b, i, "banks")]
+            ab = state[(b, i, "ab")]
+            xbs = state[(b, i, "xbs")]
+            ot = otp.tile([P, NPOS], F32)
+            for n in range(4):
+                cs = slice(n * NT, (n + 1) * NT)
+                nc.vector.scalar_tensor_tensor(out=ot[:, cs], in0=banks[n][:], scalar=ab[:, 0:1], in1=xbs[n][:],
+                                               op0=ALU.mult, op1=ALU.add)
+                if n % 2 == 1:
+                    hs_ = slice((n - 1) * NT, (n + 1) * NT)
+                    nc.sync.dma_start(out=ov[:, b, i // 2, i % 2, hs_], in_=ot[:, hs_])
+
+        def hk(k):
+            return (k // 8, (k // 2) % 4, k % 2)
+
+        x_prep(0, 0)
+        x_prep(0, 1)
+        for k in range(16):
+            b, n, g = hk(k)
+            tx = k // 2 + 2
+            mm1(b, n, g)
+            if g == 0 and tx < 8:
+                x_prep(tx // 4, tx % 4)
+            if k >= 8:
+                i = (k - 8) // 2
+                if k % 2 == 1:
+                    unit_b(0, i)
+                elif i > 0:
+                    unit_c1(0, i - 1)
+            if k > 0:
+                h_quant(*hk(k - 1))
+            if k >= 8 and k % 2 == 0:
+                i = (k - 8) // 2
+                if i > 0:
+                    unit_c2(0, i - 1)
+                unit_a(0, i)
+            if k == 3:
+                w2_prep()
+            h_regroup(b, n, g)
+        unit_c1(0, 3)
+        h_quant(1, 3, 1)
+        unit_c2(0, 3)
+        unit_a(1, 0)
+        unit_b(1, 0)
+        unit_a(1, 1)
+        unit_b(1, 1)
+        unit_c1(1, 0)
+        unit_c2(1, 0)
+        unit_a(1, 2)
+        unit_c1(1, 1)
+        unit_c2(1, 1)
+        unit_b(1, 2)
+        unit_a(1, 3)
+        unit_b(1, 3)
+        unit_c1(1, 2)
+        unit_c2(1, 2)
+        unit_c1(1, 3)
+        unit_c2(1, 3)

@@ -1,8 +1,6 @@
 from contextlib import ExitStack
 
-import concourse.bass as bass
 import concourse.mybir as mybir
-import concourse.tile as tile
 from concourse.masks import make_identity
 
 F32 = mybir.dt.float32
@@ -18,33 +16,51 @@ FLOPS = 2 * 4096 * 512 * 1024 * 2
 P = 128
 NPOS = 2048
 NT = 512
-NB = 2
 
-X_ENG = {}
-H_ENG = {(1, 0, 0): "s", (1, 0, 1): "s", (1, 1, 0): "s", (1, 1, 1): "s",
-         (1, 2, 0): "s", (1, 2, 1): "s", (1, 3, 0): "s", (1, 3, 1): "s"}
-HX_ENG = {0: "g", 1: "s"}
+X_ENG = "VVVVVVVV"
+H_ENG = "VVVVVVVVVSVSVSVS"
+FIN = "CSCSCSCSCSCSCSCSCSCSCSCSCSCSCSCS"
+W1EV = "SSSV"
+W2EV = "SVSV"
+A0 = 12
+A1 = 0
+LXR = 5
+LXQ = 3
+LW2 = 5
+LHQ = 3
+LHR = 1
+PIN = True
 
 
 def regroup(nc, eng, dst, src):
     d = dst.rearrange("p (c i) t -> p c t i", i=4)
     s = src.rearrange("p t (c i) -> p c t i", i=4)
-    if eng == "v":
+    if eng == "V":
         nc.vector.tensor_copy(out=d, in_=s)
-    elif eng == "s":
+    elif eng == "S":
         nc.scalar.copy(out=d, in_=s)
     else:
         nc.gpsimd.tensor_scalar(out=d, in0=s, scalar1=1.0, scalar2=0.0, op0=ALU.mult, op1=ALU.add)
 
 
+def evac(nc, eng, dst, src):
+    if eng == "V":
+        nc.vector.tensor_copy(out=dst, in_=src)
+    else:
+        nc.scalar.copy(out=dst, in_=src)
+
+
 def tile_axialattentionblock_pc_t_kernel(tc, x2, fc1_w, fc1_b, fc2_w, fc2_b, mlp_norm_w, gamma_mlp, out):
     nc = tc.nc
     with ExitStack() as ctx:
+        if PIN:
+            ctx.enter_context(tc.manual_schedule())
         const = ctx.enter_context(tc.tile_pool(name="const", bufs=1))
         xgp = ctx.enter_context(tc.tile_pool(name="xgp", bufs=3))
         hsp = ctx.enter_context(tc.tile_pool(name="hsp", bufs=4))
         hgp = ctx.enter_context(tc.tile_pool(name="hgp", bufs=4))
         xbp = ctx.enter_context(tc.tile_pool(name="xbp", bufs=8))
+        ttp = ctx.enter_context(tc.tile_pool(name="ttp", bufs=4))
         otp = ctx.enter_context(tc.tile_pool(name="otp", bufs=3))
         sml = ctx.enter_context(tc.tile_pool(name="sml", bufs=3))
         psa = ctx.enter_context(tc.psum_pool(name="psa", bufs=2))
@@ -59,12 +75,12 @@ def tile_axialattentionblock_pc_t_kernel(tc, x2, fc1_w, fc1_b, fc2_w, fc2_b, mlp
         nc.scalar.activation(out=warm[:], in_=zero1[:], func=ACT.Gelu)
         half = const.tile([P, 1], F32)
         nc.vector.memset(half[:], 0.5)
-        ident = const.tile([P, P], F32)
-        make_identity(nc, ident[:])
         vecs = const.tile([P, 256], BF16)
         nc.vector.memset(vecs[:], 0.0)
+        ident = const.tile([P, P], F32)
+        make_identity(nc, ident[:])
 
-        xs = [const.tile([P, 4, NPOS], BF16, name="xs%d" % b) for b in range(NB)]
+        xs = [const.tile([P, 4, NPOS], BF16, name="xs%d" % b) for b in range(2)]
         w1raw = const.tile([P, 8, 512], BF16)
         w2raw = const.tile([P, 4, 1024], BF16)
         nc.scalar.dma_start(out=vecs[0:4, :], in_=fc1_b.rearrange("(r k) -> r k", r=4))
@@ -85,7 +101,8 @@ def tile_axialattentionblock_pc_t_kernel(tc, x2, fc1_w, fc1_b, fc2_w, fc2_b, mlp
             load_x(0, n * NT, (n + 1) * NT)
         nc.sync.dma_start(out=w2raw[:].rearrange("m (u e) f -> m u (e f)", e=2),
                           in_=fc2_w.rearrange("(u m e) f -> m u (e f)", u=2, m=P, e=2))
-        load_x(1, 0, NPOS)
+        load_x(1, 0, 2 * NT)
+        load_x(1, 2 * NT, NPOS)
 
         pt = psa.tile([P, P], F32, tag="p1")
         nc.tensor.transpose(pt[:], vecs[:].bitcast(F32), ident[:])
@@ -97,64 +114,114 @@ def tile_axialattentionblock_pc_t_kernel(tc, x2, fc1_w, fc1_b, fc2_w, fc2_b, mlp
         nc.vector.tensor_tensor(out=gwb[:, :, 0], in0=prm[:, 12:16], in1=prm[:, 16:20], op=ALU.mult)
         nc.vector.tensor_tensor(out=gwb[:, :, 1], in0=gwb[:, :, 0], in1=prm[:, 8:12], op=ALU.mult)
 
-        w1g = const.tile([P, 4096], BF16, align_bytes=64)
-        w1c = const.tile([P, 1024], U32, align_bytes=64)
-        w1s = const.tile([P, 1024], U8, align_bytes=64)
-        w1g32 = w1g[:].bitcast(F32).rearrange("q (j m u) -> q j m u", j=8, m=P, u=2)
-        for jp in range(4):
-            wt = psa.tile([P, 2, 2, P], F32, tag="p1", name="wt1") if jp % 2 == 0 else psb.tile([P, 2, 2, P], F32, tag="m2", name="wt1b")
-            for jj in range(2):
-                wsrc = w1raw[:, 2 * jp + jj, :].bitcast(F32)
-                for u in range(2):
-                    nc.tensor.transpose(wt[:, jj, u, :], wsrc[:, P * u:P * u + P], ident[:])
-            src = wt[:].rearrange("q j u m -> q j m u")
-            if jp % 2 == 0:
-                nc.vector.tensor_copy(out=w1g32[:, 2 * jp:2 * jp + 2, :, :], in_=src)
-            else:
-                nc.scalar.copy(out=w1g32[:, 2 * jp:2 * jp + 2, :, :], in_=src)
-            if jp % 2 == 1:
-                h0 = (jp // 2) * 512
-                nc.vector.quantize_mx(out=w1c[:, h0:h0 + 512].bitcast(FP8X4), scales=w1s[:, h0:h0 + 512],
-                                      in_=w1g[:, 4 * h0:4 * h0 + 2048])
-
         xc = const.tile([P, 8, NT], U32, align_bytes=64)
         xsc = const.tile([P, 8, NT], U8, align_bytes=64)
         hc = const.tile([P, 16, NT], U32, align_bytes=64)
         hsc = const.tile([P, 16, NT], U8, align_bytes=64)
-
-        def x_prep(b, n):
-            xg = xgp.tile([P, NT, 4], BF16, align_bytes=64)
-            regroup(nc, X_ENG.get((b, n), "v"), xg[:], xs[b][:, :, n * NT:(n + 1) * NT])
-            k = b * 4 + n
-            nc.vector.quantize_mx(out=xc[:, k, :].bitcast(FP8X4), scales=xsc[:, k, :],
-                                  in_=xg[:].rearrange("p w t -> p (w t)"))
-
-        def mm1(b, n, g):
-            k = b * 4 + n
-            hs = hsp.tile([P, 4, NT], BF16)
-            for t in range(4):
-                j = 4 * g + t
-                p1 = psa.tile([P, NT], F32, tag="p1")
-                nc.tensor.matmul_mx(out=p1[:], lhsT=w1c[:, P * j:P * j + P].bitcast(FP8X4),
-                                    lhsT_scale=w1s[:, P * j:P * j + P],
-                                    rhs=xc[:, k, :].bitcast(FP8X4), rhs_scale=xsc[:, k, :],
-                                    start=True, stop=True)
-                nc.scalar.activation(out=hs[:, t, :], in_=p1[:], func=ACT.Gelu, bias=prm[:, j:j + 1], scale=1.0)
-            state[(b, n, g, "hs")] = hs
-
-        def h_regroup(b, n, g):
-            hg = hgp.tile([P, NT, 4], BF16, align_bytes=64)
-            regroup(nc, H_ENG.get((b, n, g), "v"), hg[:], state[(b, n, g, "hs")][:])
-            state[(b, n, g, "hg")] = hg
-
-        def h_quant(b, n, g):
-            k = b * 4 + n
-            nc.vector.quantize_mx(out=hc[:, 2 * k + g, :].bitcast(FP8X4), scales=hsc[:, 2 * k + g, :],
-                                  in_=state[(b, n, g, "hg")][:].rearrange("p w t -> p (w t)"))
-
+        w1g = const.tile([P, 4096], BF16, align_bytes=64)
+        w1c = const.tile([P, 1024], U32, align_bytes=64)
+        w1s = const.tile([P, 1024], U8, align_bytes=64)
         w2g = const.tile([P, 4096], BF16, align_bytes=64)
         w2c = const.tile([P, 2, 512], U32, align_bytes=64)
         w2s = const.tile([P, 2, 512], U8, align_bytes=64)
+        st = {}
+
+        def x_regroup(q):
+            xg = xgp.tile([P, NT, 4], BF16, align_bytes=64, name="xg")
+            regroup(nc, X_ENG[q], xg[:], xs[q // 4][:, :, (q % 4) * NT:(q % 4 + 1) * NT])
+            st[("xg", q)] = xg
+
+        def x_quant(q):
+            nc.vector.quantize_mx(out=xc[:, q, :].bitcast(FP8X4), scales=xsc[:, q, :],
+                                  in_=st[("xg", q)][:].rearrange("p w t -> p (w t)"))
+
+        def mm1_gelu(k):
+            q = k // 2
+            g = k % 2
+            hs = hsp.tile([P, 4, NT], BF16, name="hs")
+            for t in range(4):
+                j = 4 * g + t
+                p1 = psa.tile([P, NT], F32, tag="p1", name="p1")
+                nc.tensor.matmul_mx(out=p1[:], lhsT=w1c[:, P * j:P * j + P].bitcast(FP8X4),
+                                    lhsT_scale=w1s[:, P * j:P * j + P],
+                                    rhs=xc[:, q, :].bitcast(FP8X4), rhs_scale=xsc[:, q, :],
+                                    start=True, stop=True)
+                nc.scalar.activation(out=hs[:, t, :], in_=p1[:], func=ACT.Gelu, bias=prm[:, j:j + 1], scale=1.0)
+            st[("hs", k)] = hs
+
+        def h_regroup(k):
+            hg = hgp.tile([P, NT, 4], BF16, align_bytes=64, name="hg")
+            regroup(nc, H_ENG[k], hg[:], st[("hs", k)][:])
+            st[("hg", k)] = hg
+
+        def h_quant(k):
+            nc.vector.quantize_mx(out=hc[:, k, :].bitcast(FP8X4), scales=hsc[:, k, :],
+                                  in_=st[("hg", k)][:].rearrange("p w t -> p (w t)"))
+
+        def mm2(v, n):
+            i = v % 4
+            k = ((v // 4) * 4 + n) * 2
+            m2 = psb.tile([P, NT], F32, tag="m2", name="m2")
+            for g in range(2):
+                nc.tensor.matmul_mx(out=m2[:], lhsT=w2c[:, g, P * i:P * i + P].bitcast(FP8X4),
+                                    lhsT_scale=w2s[:, g, P * i:P * i + P],
+                                    rhs=hc[:, k + g, :].bitcast(FP8X4), rhs_scale=hsc[:, k + g, :],
+                                    start=(g == 0), stop=(g == 1))
+            st[("m2", v, n)] = m2
+
+        def stats(v, n):
+            if n == 0:
+                st[("st", v)] = sml.tile([P, 4, 6], F32, name="bst")
+            nc.vector.bn_stats(out=st[("st", v)][:, n, :], in_=st[("m2", v, n)][:])
+
+        def chain1(v):
+            mv = sml.tile([P, 2], F32, name="mv")
+            nc.vector.bn_aggr(out=mv[:], in_=st[("st", v)][:].rearrange("p n s -> p (n s)"))
+            sd = sml.tile([P, 1], F32, name="sd")
+            nc.gpsimd.tensor_tensor(out=sd[:], in0=mv[:, 1:2], in1=half[:], op=ALU.pow)
+            st[("sd", v)] = sd
+
+        def chain2(v):
+            se = sml.tile([P, 1], F32, name="se")
+            nc.vector.tensor_scalar(out=se[:], in0=st[("sd", v)][:], scalar1=(NPOS / (NPOS - 1.0)) ** 0.5, scalar2=1e-8,
+                                    op0=ALU.mult, op1=ALU.add)
+            rc = sml.tile([P, 1], F32, name="rc")
+            nc.vector.reciprocal(out=rc[:], in_=se[:])
+            ab = sml.tile([P, 2], F32, name="ab")
+            nc.vector.tensor_scalar(out=ab[:], in0=gwb[:, v % 4, :], scalar1=rc[:, 0:1], scalar2=None, op0=ALU.mult)
+            st[("ab", v)] = ab
+
+        def pre(v, n):
+            m = FIN[4 * v + n]
+            ab = st[("ab", v)]
+            xsl = xs[v // 4][:, v % 4, n * NT:(n + 1) * NT]
+            if m == "C":
+                tt = ttp.tile([P, NT], F32, name="tt")
+                nc.scalar.activation(out=tt[:], in_=st[("m2", v, n)][:], func=ACT.Identity, bias=ab[:, 1:2], scale=ab[:, 0:1])
+                st[("tt", v, n)] = tt
+            else:
+                xb = xbp.tile([P, NT], F32, name="xb")
+                if m == "G":
+                    nc.gpsimd.tensor_scalar(out=xb[:], in0=xsl, scalar1=1.0, scalar2=ab[:, 1:2], op0=ALU.mult, op1=ALU.add)
+                else:
+                    nc.scalar.activation(out=xb[:], in_=xsl, func=ACT.Identity, bias=ab[:, 1:2], scale=1.0)
+                st[("xb", v, n)] = xb
+
+        def final(v, n):
+            m = FIN[4 * v + n]
+            if n == 0:
+                st[("ot", v)] = otp.tile([P, NPOS], F32, name="ot")
+            ot = st[("ot", v)]
+            cs = slice(n * NT, (n + 1) * NT)
+            if m == "C":
+                nc.gpsimd.tensor_tensor(out=ot[:, cs], in0=st[("tt", v, n)][:], in1=xs[v // 4][:, v % 4, cs], op=ALU.add)
+            else:
+                nc.vector.scalar_tensor_tensor(out=ot[:, cs], in0=st[("m2", v, n)][:], scalar=st[("ab", v)][:, 0:1],
+                                               in1=st[("xb", v, n)][:], op0=ALU.mult, op1=ALU.add)
+            if n % 2 == 1:
+                c2 = slice((n - 1) * NT, (n + 1) * NT)
+                i = v % 4
+                nc.sync.dma_start(out=ov[:, v // 4, i // 2, i % 2, c2], in_=ot[:, c2])
 
         def w2_prep():
             w2g32 = w2g[:].bitcast(F32).rearrange("q (g i m u) -> q g i m u", g=2, i=4, m=P, u=2)
@@ -163,119 +230,76 @@ def tile_axialattentionblock_pc_t_kernel(tc, x2, fc1_w, fc1_b, fc2_w, fc2_b, mlp
                 wsrc = w2raw[:, i, :].bitcast(F32)
                 for r in range(4):
                     nc.tensor.transpose(wt[:, r, :], wsrc[:, P * r:P * r + P], ident[:])
-                src = wt[:].rearrange("q (g u) m -> q g m u", g=2)
-                if i % 2 == 0:
-                    nc.vector.tensor_copy(out=w2g32[:, :, i, :, :], in_=src)
-                else:
-                    nc.scalar.copy(out=w2g32[:, :, i, :, :], in_=src)
+                evac(nc, W2EV[i], w2g32[:, :, i, :, :], wt[:].rearrange("q (g u) m -> q g m u", g=2))
             for g in range(2):
                 nc.vector.quantize_mx(out=w2c[:, g, :].bitcast(FP8X4), scales=w2s[:, g, :],
                                       in_=w2g[:, 2048 * g:2048 * g + 2048])
 
-        state = {}
+        x_regroup(0)
+        w1g32 = w1g[:].bitcast(F32).rearrange("q (j m u) -> q j m u", j=8, m=P, u=2)
+        for jp in range(4):
+            if jp % 2 == 0:
+                wt = psa.tile([P, 2, 2, P], F32, tag="p1", name="wt1")
+            else:
+                wt = psb.tile([P, 2, 2, P], F32, tag="m2", name="wt1b")
+            for jj in range(2):
+                wsrc = w1raw[:, 2 * jp + jj, :].bitcast(F32)
+                for u in range(2):
+                    nc.tensor.transpose(wt[:, jj, u, :], wsrc[:, P * u:P * u + P], ident[:])
+            evac(nc, W1EV[jp], w1g32[:, 2 * jp:2 * jp + 2, :, :], wt[:].rearrange("q j u m -> q j m u"))
+            if jp == 0:
+                x_quant(0)
+            if jp % 2 == 1:
+                h0 = (jp // 2) * 512
+                nc.vector.quantize_mx(out=w1c[:, h0:h0 + 512].bitcast(FP8X4), scales=w1s[:, h0:h0 + 512],
+                                      in_=w1g[:, 4 * h0:4 * h0 + 2048])
 
-        def unit_a(b, i):
-            banks = []
-            for n in range(4):
-                k = b * 4 + n
-                m2 = psb.tile([P, NT], F32, tag="m2", name="m2")
-                for g in range(2):
-                    nc.tensor.matmul_mx(out=m2[:], lhsT=w2c[:, g, P * i:P * i + P].bitcast(FP8X4),
-                                        lhsT_scale=w2s[:, g, P * i:P * i + P],
-                                        rhs=hc[:, 2 * k + g, :].bitcast(FP8X4), rhs_scale=hsc[:, 2 * k + g, :],
-                                        start=(g == 0), stop=(g == 1))
-                banks.append(m2)
-            state[(b, i, "banks")] = banks
+        def a_of(v):
+            return A0 + 2 * v + (A1 if v >= 4 else 0)
 
-        def unit_b(b, i):
-            banks = state[(b, i, "banks")]
-            st = sml.tile([P, 4, 6], F32)
-            for n in range(4):
-                nc.vector.bn_stats(out=st[:, n, :], in_=banks[n][:])
-            mv = sml.tile([P, 2], F32)
-            nc.vector.bn_aggr(out=mv[:], in_=st[:].rearrange("p n s -> p (n s)"))
-            sd = sml.tile([P, 1], F32)
-            nc.gpsimd.tensor_tensor(out=sd[:], in0=mv[:, 1:2], in1=half[:], op=ALU.pow)
-            state[(b, i, "sd")] = sd
-
-        def unit_c1(b, i):
-            sd = state[(b, i, "sd")]
-            se = sml.tile([P, 1], F32)
-            nc.vector.tensor_scalar(out=se[:], in0=sd[:], scalar1=(NPOS / (NPOS - 1.0)) ** 0.5, scalar2=1e-8,
-                                    op0=ALU.mult, op1=ALU.add)
-            rc = sml.tile([P, 1], F32)
-            nc.vector.reciprocal(out=rc[:], in_=se[:])
-            ab = sml.tile([P, 2], F32)
-            nc.vector.tensor_scalar(out=ab[:], in0=gwb[:, i, :], scalar1=rc[:, 0:1], scalar2=None, op0=ALU.mult)
-            xbs = []
-            for n in range(4):
-                cs = slice(n * NT, (n + 1) * NT)
-                xb = xbp.tile([P, NT], F32, name="xb")
-                if HX_ENG[b] == "g":
-                    nc.gpsimd.tensor_scalar(out=xb[:], in0=xs[b][:, i, cs], scalar1=1.0, scalar2=ab[:, 1:2],
-                                            op0=ALU.mult, op1=ALU.add)
-                else:
-                    nc.scalar.activation(out=xb[:], in_=xs[b][:, i, cs], func=ACT.Identity, bias=ab[:, 1:2], scale=1.0)
-                xbs.append(xb)
-            state[(b, i, "ab")] = ab
-            state[(b, i, "xbs")] = xbs
-
-        def unit_c2(b, i):
-            banks = state[(b, i, "banks")]
-            ab = state[(b, i, "ab")]
-            xbs = state[(b, i, "xbs")]
-            ot = otp.tile([P, NPOS], F32)
-            for n in range(4):
-                cs = slice(n * NT, (n + 1) * NT)
-                nc.vector.scalar_tensor_tensor(out=ot[:, cs], in0=banks[n][:], scalar=ab[:, 0:1], in1=xbs[n][:],
-                                               op0=ALU.mult, op1=ALU.add)
-                if n % 2 == 1:
-                    hs_ = slice((n - 1) * NT, (n + 1) * NT)
-                    nc.sync.dma_start(out=ov[:, b, i // 2, i % 2, hs_], in_=ot[:, hs_])
-
-        def hk(k):
-            return (k // 8, (k // 2) % 4, k % 2)
-
-        x_prep(0, 0)
-        x_prep(0, 1)
-        for k in range(16):
-            b, n, g = hk(k)
-            tx = k // 2 + 2
-            mm1(b, n, g)
-            if g == 0 and tx < 8:
-                x_prep(tx // 4, tx % 4)
-            if k >= 8:
-                i = (k - 8) // 2
-                if k % 2 == 1:
-                    unit_b(0, i)
-                elif i > 0:
-                    unit_c1(0, i - 1)
-            if k > 0:
-                h_quant(*hk(k - 1))
-            if k >= 8 and k % 2 == 0:
-                i = (k - 8) // 2
-                if i > 0:
-                    unit_c2(0, i - 1)
-                unit_a(0, i)
-            if k == 3:
+        units = range(8)
+        for w in range(-4, 44):
+            for q in range(1, 8):
+                if 2 * q - LXR == w or (w == -4 and 2 * q - LXR < -4):
+                    x_regroup(q)
+            if 0 <= w < 16:
+                mm1_gelu(w)
+            for q in range(1, 8):
+                if 2 * q - LXQ == w or (w == -4 and 2 * q - LXQ < -4):
+                    x_quant(q)
+            if w == LW2:
                 w2_prep()
-            h_regroup(b, n, g)
-        unit_c1(0, 3)
-        h_quant(1, 3, 1)
-        unit_c2(0, 3)
-        unit_a(1, 0)
-        unit_b(1, 0)
-        unit_a(1, 1)
-        unit_b(1, 1)
-        unit_c1(1, 0)
-        unit_c2(1, 0)
-        unit_a(1, 2)
-        unit_c1(1, 1)
-        unit_c2(1, 1)
-        unit_b(1, 2)
-        unit_a(1, 3)
-        unit_b(1, 3)
-        unit_c1(1, 2)
-        unit_c2(1, 2)
-        unit_c1(1, 3)
-        unit_c2(1, 3)
+            for v in units:
+                if w == a_of(v):
+                    stats(v, 0)
+                    stats(v, 1)
+            for v in units:
+                if w == a_of(v) + 2:
+                    final(v, 0)
+                    final(v, 1)
+            for v in units:
+                if w == a_of(v):
+                    mm2(v, 2)
+                    mm2(v, 3)
+            if 0 <= w - LHQ < 16:
+                h_quant(w - LHQ)
+            for v in units:
+                if w == a_of(v) + 1:
+                    stats(v, 2)
+                    stats(v, 3)
+                    chain1(v)
+            for v in units:
+                if w == a_of(v) + 3:
+                    final(v, 2)
+                    final(v, 3)
+            for v in units:
+                if w == a_of(v) - 1:
+                    mm2(v, 0)
+                    mm2(v, 1)
+            for v in units:
+                if w == a_of(v) + 1:
+                    chain2(v)
+                    for n in range(4):
+                        pre(v, n)
+            if 0 <= w - LHR < 16:
+                h_regroup(w - LHR)

@@ -16,20 +16,22 @@ FLOPS = 2 * 4096 * 512 * 1024 * 2
 P = 128
 NPOS = 2048
 NT = 512
+TILES = 8
+HALVES = 2 * TILES
 
 X_ENG = "VVVVVVVV"
-H_ENG = "VVVVVVVVVSVSVSVS"
-FIN = "CSCSCSCSCSCSCSCSCSCSCSCSCSCSCSCS"
-W1EV = "SSSV"
-W2EV = "SVSV"
-A0 = 12
-A1 = 0
+H_ENG = "VVVVVVVVVVVVVVVV"
 LXR = 5
 LXQ = 3
-LW2 = 5
-LHQ = 3
+LW2 = 3
 LHR = 1
-PIN = True
+LHQ = 2
+LM2 = 3
+LBN = 4
+LC2 = 1
+FS = (1, 0, 0)
+FT = (1, 1, 1)
+TAILW = 16
 
 
 def regroup(nc, eng, dst, src):
@@ -53,18 +55,17 @@ def evac(nc, eng, dst, src):
 def tile_axialattentionblock_pc_t_kernel(tc, x2, fc1_w, fc1_b, fc2_w, fc2_b, mlp_norm_w, gamma_mlp, out):
     nc = tc.nc
     with ExitStack() as ctx:
-        if PIN:
-            ctx.enter_context(tc.manual_schedule())
+        ctx.enter_context(tc.manual_schedule())
         const = ctx.enter_context(tc.tile_pool(name="const", bufs=1))
         xgp = ctx.enter_context(tc.tile_pool(name="xgp", bufs=3))
+        xcp = ctx.enter_context(tc.tile_pool(name="xcp", bufs=3))
         hsp = ctx.enter_context(tc.tile_pool(name="hsp", bufs=4))
         hgp = ctx.enter_context(tc.tile_pool(name="hgp", bufs=4))
-        xbp = ctx.enter_context(tc.tile_pool(name="xbp", bufs=8))
-        ttp = ctx.enter_context(tc.tile_pool(name="ttp", bufs=4))
-        otp = ctx.enter_context(tc.tile_pool(name="otp", bufs=3))
-        sml = ctx.enter_context(tc.tile_pool(name="sml", bufs=3))
-        psa = ctx.enter_context(tc.psum_pool(name="psa", bufs=2))
-        psb = ctx.enter_context(tc.psum_pool(name="psb", bufs=6))
+        hcp = ctx.enter_context(tc.tile_pool(name="hcp", bufs=4))
+        msp = ctx.enter_context(tc.tile_pool(name="msp", bufs=8))
+        sml = ctx.enter_context(tc.tile_pool(name="sml", bufs=2))
+        psa = ctx.enter_context(tc.psum_pool(name="psa", bufs=4))
+        psb = ctx.enter_context(tc.psum_pool(name="psb", bufs=4))
 
         xv = x2.rearrange("b (u q e) h w -> q b u e (h w)", u=2, q=P, e=2)
         ov = out.rearrange("b (u q e) h w -> q b u e (h w)", u=2, q=P, e=2)
@@ -73,7 +74,7 @@ def tile_axialattentionblock_pc_t_kernel(tc, x2, fc1_w, fc1_b, fc2_w, fc2_b, mlp
         nc.vector.memset(zero1[:], 0.0)
         warm = const.tile([P, 1], F32)
         nc.scalar.activation(out=warm[:], in_=zero1[:], func=ACT.Gelu)
-        half = const.tile([P, 1], F32)
+        half = const.tile([P, 4], F32)
         nc.vector.memset(half[:], 0.5)
         vecs = const.tile([P, 256], BF16)
         nc.vector.memset(vecs[:], 0.0)
@@ -97,10 +98,10 @@ def tile_axialattentionblock_pc_t_kernel(tc, x2, fc1_w, fc1_b, fc2_w, fc2_b, mlp
         load_x(0, 0, NT)
         nc.sync.dma_start(out=w1r[:, 0:2, :], in_=w1d[:, 0:2, :])
         nc.sync.dma_start(out=w1r[:, 2:4, :], in_=w1d[:, 2:4, :])
-        for n in range(1, 4):
-            load_x(0, n * NT, (n + 1) * NT)
+        load_x(0, NT, 2 * NT)
         nc.sync.dma_start(out=w2raw[:].rearrange("m (u e) f -> m u (e f)", e=2),
                           in_=fc2_w.rearrange("(u m e) f -> m u (e f)", u=2, m=P, e=2))
+        load_x(0, 2 * NT, NPOS)
         load_x(1, 0, 2 * NT)
         load_x(1, 2 * NT, NPOS)
 
@@ -110,18 +111,11 @@ def tile_axialattentionblock_pc_t_kernel(tc, x2, fc1_w, fc1_b, fc2_w, fc2_b, mlp
         nc.vector.tensor_copy(out=prw[:, 0:10], in_=pt[:, 0:10])
         prm = const.tile([P, 20], F32)
         nc.vector.tensor_copy(out=prm[:], in_=prw[:, 0:10].bitcast(BF16))
-        gwb = const.tile([P, 4, 2], F32)
-        nc.vector.tensor_tensor(out=gwb[:, :, 0], in0=prm[:, 12:16], in1=prm[:, 16:20], op=ALU.mult)
-        nc.vector.tensor_tensor(out=gwb[:, :, 1], in0=gwb[:, :, 0], in1=prm[:, 8:12], op=ALU.mult)
+        gw = const.tile([P, 4], F32)
+        nc.vector.tensor_tensor(out=gw[:], in0=prm[:, 12:16], in1=prm[:, 16:20], op=ALU.mult)
 
-        xc = const.tile([P, 8, NT], U32, align_bytes=64)
-        xsc = const.tile([P, 8, NT], U8, align_bytes=64)
-        hc = const.tile([P, 16, NT], U32, align_bytes=64)
-        hsc = const.tile([P, 16, NT], U8, align_bytes=64)
-        w1g = const.tile([P, 4096], BF16, align_bytes=64)
         w1c = const.tile([P, 1024], U32, align_bytes=64)
         w1s = const.tile([P, 1024], U8, align_bytes=64)
-        w2g = const.tile([P, 4096], BF16, align_bytes=64)
         w2c = const.tile([P, 2, 512], U32, align_bytes=64)
         w2s = const.tile([P, 2, 512], U8, align_bytes=64)
         st = {}
@@ -132,11 +126,13 @@ def tile_axialattentionblock_pc_t_kernel(tc, x2, fc1_w, fc1_b, fc2_w, fc2_b, mlp
             st[("xg", q)] = xg
 
         def x_quant(q):
-            nc.vector.quantize_mx(out=xc[:, q, :].bitcast(FP8X4), scales=xsc[:, q, :],
-                                  in_=st[("xg", q)][:].rearrange("p w t -> p (w t)"))
+            xc = xcp.tile([P, NT], U32, align_bytes=64, name="xc")
+            xsc = xcp.tile([P, NT], U8, align_bytes=64, name="xsc")
+            nc.vector.quantize_mx(out=xc[:].bitcast(FP8X4), scales=xsc[:], in_=st[("xg", q)][:].rearrange("p w t -> p (w t)"))
+            st[("xc", q)] = (xc, xsc)
 
         def mm1_gelu(k):
-            q = k // 2
+            xc, xsc = st[("xc", k // 2)]
             g = k % 2
             hs = hsp.tile([P, 4, NT], BF16, name="hs")
             for t in range(4):
@@ -144,8 +140,7 @@ def tile_axialattentionblock_pc_t_kernel(tc, x2, fc1_w, fc1_b, fc2_w, fc2_b, mlp
                 p1 = psa.tile([P, NT], F32, tag="p1", name="p1")
                 nc.tensor.matmul_mx(out=p1[:], lhsT=w1c[:, P * j:P * j + P].bitcast(FP8X4),
                                     lhsT_scale=w1s[:, P * j:P * j + P],
-                                    rhs=xc[:, q, :].bitcast(FP8X4), rhs_scale=xsc[:, q, :],
-                                    start=True, stop=True)
+                                    rhs=xc[:].bitcast(FP8X4), rhs_scale=xsc[:], start=True, stop=True)
                 nc.scalar.activation(out=hs[:, t, :], in_=p1[:], func=ACT.Gelu, bias=prm[:, j:j + 1], scale=1.0)
             st[("hs", k)] = hs
 
@@ -155,87 +150,77 @@ def tile_axialattentionblock_pc_t_kernel(tc, x2, fc1_w, fc1_b, fc2_w, fc2_b, mlp
             st[("hg", k)] = hg
 
         def h_quant(k):
-            nc.vector.quantize_mx(out=hc[:, k, :].bitcast(FP8X4), scales=hsc[:, k, :],
+            if k % 2 == 0:
+                st[("hc", k // 2)] = (hcp.tile([P, 2, NT], U32, align_bytes=64, name="hc"),
+                                      hcp.tile([P, 2, NT], U8, align_bytes=64, name="hsc"))
+            hc, hsc = st[("hc", k // 2)]
+            nc.vector.quantize_mx(out=hc[:, k % 2, :].bitcast(FP8X4), scales=hsc[:, k % 2, :],
                                   in_=st[("hg", k)][:].rearrange("p w t -> p (w t)"))
 
-        def mm2(v, n):
-            i = v % 4
-            k = ((v // 4) * 4 + n) * 2
+        def mm2_evac(q, i):
+            hc, hsc = st[("hc", q)]
+            b = q // 4
+            n = q % 4
             m2 = psb.tile([P, NT], F32, tag="m2", name="m2")
             for g in range(2):
                 nc.tensor.matmul_mx(out=m2[:], lhsT=w2c[:, g, P * i:P * i + P].bitcast(FP8X4),
                                     lhsT_scale=w2s[:, g, P * i:P * i + P],
-                                    rhs=hc[:, k + g, :].bitcast(FP8X4), rhs_scale=hsc[:, k + g, :],
+                                    rhs=hc[:, g, :].bitcast(FP8X4), rhs_scale=hsc[:, g, :],
                                     start=(g == 0), stop=(g == 1))
-            st[("m2", v, n)] = m2
-
-        def stats(v, n):
             if n == 0:
-                st[("st", v)] = sml.tile([P, 4, 6], F32, name="bst")
-            nc.vector.bn_stats(out=st[("st", v)][:, n, :], in_=st[("m2", v, n)][:])
+                st[("m", b, i)] = msp.tile([P, NPOS], F32, name="m")
+            nc.scalar.activation(out=st[("m", b, i)][:, n * NT:(n + 1) * NT], in_=m2[:], func=ACT.Identity,
+                                 bias=prm[:, 8 + i:9 + i], scale=1.0)
 
-        def chain1(v):
-            mv = sml.tile([P, 2], F32, name="mv")
-            nc.vector.bn_aggr(out=mv[:], in_=st[("st", v)][:].rearrange("p n s -> p (n s)"))
-            sd = sml.tile([P, 1], F32, name="sd")
-            nc.gpsimd.tensor_tensor(out=sd[:], in0=mv[:, 1:2], in1=half[:], op=ALU.pow)
-            st[("sd", v)] = sd
+        def stats(q, i):
+            b = q // 4
+            n = q % 4
+            if n == 0 and i == 0:
+                st[("bst", b)] = sml.tile([P, 4, 4, 6], F32, name="bst")
+            nc.vector.bn_stats(out=st[("bst", b)][:, i, n, :], in_=st[("m", b, i)][:, n * NT:(n + 1) * NT])
 
-        def chain2(v):
-            se = sml.tile([P, 1], F32, name="se")
-            nc.vector.tensor_scalar(out=se[:], in0=st[("sd", v)][:], scalar1=(NPOS / (NPOS - 1.0)) ** 0.5, scalar2=1e-8,
+        def chain1(b):
+            mv = sml.tile([P, 4, 2], F32, name="mv")
+            for i in range(4):
+                nc.vector.bn_aggr(out=mv[:, i, :], in_=st[("bst", b)][:, i, :, :].rearrange("p n s -> p (n s)"))
+            sd = sml.tile([P, 4], F32, name="sd")
+            nc.gpsimd.tensor_tensor(out=sd[:], in0=mv[:, :, 1], in1=half[:], op=ALU.pow)
+            st[("sd", b)] = sd
+
+        def chain2(b):
+            se = sml.tile([P, 4], F32, name="se")
+            nc.vector.tensor_scalar(out=se[:], in0=st[("sd", b)][:], scalar1=(NPOS / (NPOS - 1.0)) ** 0.5, scalar2=1e-8,
                                     op0=ALU.mult, op1=ALU.add)
-            rc = sml.tile([P, 1], F32, name="rc")
+            rc = sml.tile([P, 4], F32, name="rc")
             nc.vector.reciprocal(out=rc[:], in_=se[:])
-            ab = sml.tile([P, 2], F32, name="ab")
-            nc.vector.tensor_scalar(out=ab[:], in0=gwb[:, v % 4, :], scalar1=rc[:, 0:1], scalar2=None, op0=ALU.mult)
-            st[("ab", v)] = ab
+            av = sml.tile([P, 4], F32, name="av")
+            nc.vector.tensor_tensor(out=av[:], in0=rc[:], in1=gw[:], op=ALU.mult)
+            st[("av", b)] = av
 
-        def pre(v, n):
-            m = FIN[4 * v + n]
-            ab = st[("ab", v)]
-            xsl = xs[v // 4][:, v % 4, n * NT:(n + 1) * NT]
-            if m == "C":
-                tt = ttp.tile([P, NT], F32, name="tt")
-                nc.scalar.activation(out=tt[:], in_=st[("m2", v, n)][:], func=ACT.Identity, bias=ab[:, 1:2], scale=ab[:, 0:1])
-                st[("tt", v, n)] = tt
-            else:
-                xb = xbp.tile([P, NT], F32, name="xb")
-                if m == "G":
-                    nc.gpsimd.tensor_scalar(out=xb[:], in0=xsl, scalar1=1.0, scalar2=ab[:, 1:2], op0=ALU.mult, op1=ALU.add)
-                else:
-                    nc.scalar.activation(out=xb[:], in_=xsl, func=ACT.Identity, bias=ab[:, 1:2], scale=1.0)
-                st[("xb", v, n)] = xb
-
-        def final(v, n):
-            m = FIN[4 * v + n]
-            if n == 0:
-                st[("ot", v)] = otp.tile([P, NPOS], F32, name="ot")
-            ot = st[("ot", v)]
+        def final(b, i, n):
+            m = st[("m", b, i)]
             cs = slice(n * NT, (n + 1) * NT)
-            if m == "C":
-                nc.gpsimd.tensor_tensor(out=ot[:, cs], in0=st[("tt", v, n)][:], in1=xs[v // 4][:, v % 4, cs], op=ALU.add)
-            else:
-                nc.vector.scalar_tensor_tensor(out=ot[:, cs], in0=st[("m2", v, n)][:], scalar=st[("ab", v)][:, 0:1],
-                                               in1=st[("xb", v, n)][:], op0=ALU.mult, op1=ALU.add)
+            nc.vector.scalar_tensor_tensor(out=m[:, cs], in0=m[:, cs], scalar=st[("av", b)][:, i:i + 1],
+                                           in1=xs[b][:, i, cs], op0=ALU.mult, op1=ALU.add)
             if n % 2 == 1:
                 c2 = slice((n - 1) * NT, (n + 1) * NT)
-                i = v % 4
-                nc.sync.dma_start(out=ov[:, v // 4, i // 2, i % 2, c2], in_=ot[:, c2])
+                nc.sync.dma_start(out=ov[:, b, i // 2, i % 2, c2], in_=m[:, c2])
 
         def w2_prep():
+            w2g = const.tile([P, 4096], BF16, align_bytes=64, tag="wg", name="w2g")
             w2g32 = w2g[:].bitcast(F32).rearrange("q (g i m u) -> q g i m u", g=2, i=4, m=P, u=2)
             for i in range(4):
                 wt = psb.tile([P, 4, P], F32, tag="m2", name="wt2")
                 wsrc = w2raw[:, i, :].bitcast(F32)
                 for r in range(4):
                     nc.tensor.transpose(wt[:, r, :], wsrc[:, P * r:P * r + P], ident[:])
-                evac(nc, W2EV[i], w2g32[:, :, i, :, :], wt[:].rearrange("q (g u) m -> q g m u", g=2))
+                evac(nc, "SVSV"[i], w2g32[:, :, i, :, :], wt[:].rearrange("q (g u) m -> q g m u", g=2))
             for g in range(2):
                 nc.vector.quantize_mx(out=w2c[:, g, :].bitcast(FP8X4), scales=w2s[:, g, :],
                                       in_=w2g[:, 2048 * g:2048 * g + 2048])
 
         x_regroup(0)
+        w1g = const.tile([P, 4096], BF16, align_bytes=64, tag="wg", name="w1g")
         w1g32 = w1g[:].bitcast(F32).rearrange("q (j m u) -> q j m u", j=8, m=P, u=2)
         for jp in range(4):
             if jp % 2 == 0:
@@ -246,7 +231,7 @@ def tile_axialattentionblock_pc_t_kernel(tc, x2, fc1_w, fc1_b, fc2_w, fc2_b, mlp
                 wsrc = w1raw[:, 2 * jp + jj, :].bitcast(F32)
                 for u in range(2):
                     nc.tensor.transpose(wt[:, jj, u, :], wsrc[:, P * u:P * u + P], ident[:])
-            evac(nc, W1EV[jp], w1g32[:, 2 * jp:2 * jp + 2, :, :], wt[:].rearrange("q j u m -> q j m u"))
+            evac(nc, "SSSV"[jp], w1g32[:, 2 * jp:2 * jp + 2, :, :], wt[:].rearrange("q j u m -> q j m u"))
             if jp == 0:
                 x_quant(0)
             if jp % 2 == 1:
@@ -254,52 +239,44 @@ def tile_axialattentionblock_pc_t_kernel(tc, x2, fc1_w, fc1_b, fc2_w, fc2_b, mlp
                 nc.vector.quantize_mx(out=w1c[:, h0:h0 + 512].bitcast(FP8X4), scales=w1s[:, h0:h0 + 512],
                                       in_=w1g[:, 4 * h0:4 * h0 + 2048])
 
-        def a_of(v):
-            return A0 + 2 * v + (A1 if v >= 4 else 0)
+        todo = []
 
-        units = range(8)
-        for w in range(-4, 44):
-            for q in range(1, 8):
+        def finals(count):
+            for c in range(count):
+                if todo:
+                    final(*todo.pop(0))
+
+        for w in range(-4, HALVES + TAILW):
+            rate = FS if w < HALVES else FT
+            for q in range(1, TILES):
                 if 2 * q - LXR == w or (w == -4 and 2 * q - LXR < -4):
                     x_regroup(q)
-            if 0 <= w < 16:
+            if 0 <= w < HALVES:
                 mm1_gelu(w)
-            for q in range(1, 8):
-                if 2 * q - LXQ == w or (w == -4 and 2 * q - LXQ < -4):
-                    x_quant(q)
             if w == LW2:
                 w2_prep()
-            for v in units:
-                if w == a_of(v):
-                    stats(v, 0)
-                    stats(v, 1)
-            for v in units:
-                if w == a_of(v) + 2:
-                    final(v, 0)
-                    final(v, 1)
-            for v in units:
-                if w == a_of(v):
-                    mm2(v, 2)
-                    mm2(v, 3)
-            if 0 <= w - LHQ < 16:
-                h_quant(w - LHQ)
-            for v in units:
-                if w == a_of(v) + 1:
-                    stats(v, 2)
-                    stats(v, 3)
-                    chain1(v)
-            for v in units:
-                if w == a_of(v) + 3:
-                    final(v, 2)
-                    final(v, 3)
-            for v in units:
-                if w == a_of(v) - 1:
-                    mm2(v, 0)
-                    mm2(v, 1)
-            for v in units:
-                if w == a_of(v) + 1:
-                    chain2(v)
-                    for n in range(4):
-                        pre(v, n)
-            if 0 <= w - LHR < 16:
+            for q in range(TILES):
+                if w == 2 * q + 1 + LM2:
+                    for i in range(4):
+                        mm2_evac(q, i)
+            if 0 <= w - LHR < HALVES:
                 h_regroup(w - LHR)
+            for q in range(1, TILES):
+                if 2 * q - LXQ == w or (w == -4 and 2 * q - LXQ < -4):
+                    x_quant(q)
+            finals(rate[0])
+            if 0 <= w - LHQ < HALVES:
+                h_quant(w - LHQ)
+            finals(rate[1])
+            for q in range(TILES):
+                if w == 2 * q + 1 + LBN:
+                    for i in range(4):
+                        stats(q, i)
+                    if q % 4 == 3:
+                        chain1(q // 4)
+            finals(rate[2])
+            for b in range(2):
+                if w == 2 * (4 * b + 3) + 1 + LBN + LC2:
+                    chain2(b)
+                    todo.extend([(b, i, n) for i in range(4) for n in range(4)])
+        finals(len(todo))

@@ -20,17 +20,17 @@ TILES = 8
 HALVES = 2 * TILES
 
 X_ENG = "VVVVVVVV"
-H_ENG = "VVVVVVVVVVVVVVVV"
-LXR = 5
-LXQ = 3
+H_ENG = "VVVSVVVSVVVSVVVS"
+LXR = 4
+LXQ = 2
 LW2 = 3
 LHR = 1
 LHQ = 2
 LM2 = 3
 LBN = 4
 LC2 = 1
-FS = (1, 0, 0)
-FT = (1, 1, 1)
+FS = (0, 0, 1)
+FT = (0, 0, 1)
 TAILW = 16
 
 
@@ -70,59 +70,51 @@ def tile_axialattentionblock_pc_t_kernel(tc, x2, fc1_w, fc1_b, fc2_w, fc2_b, mlp
         xv = x2.rearrange("b (u q e) h w -> q b u e (h w)", u=2, q=P, e=2)
         ov = out.rearrange("b (u q e) h w -> q b u e (h w)", u=2, q=P, e=2)
 
+        vecs = const.tile([P, 256], BF16)
+        nc.vector.memset(vecs[:], 0.0)
         zero1 = const.tile([P, 1], F32)
         nc.vector.memset(zero1[:], 0.0)
         warm = const.tile([P, 1], F32)
         nc.scalar.activation(out=warm[:], in_=zero1[:], func=ACT.Gelu)
         half = const.tile([P, 4], F32)
         nc.vector.memset(half[:], 0.5)
-        vecs = const.tile([P, 256], BF16)
-        nc.vector.memset(vecs[:], 0.0)
         ident = const.tile([P, P], F32)
         make_identity(nc, ident[:])
 
-        xs = [const.tile([P, 4, NPOS], BF16, name="xs%d" % b) for b in range(2)]
+        xs = [const.tile([P, 4, NT], BF16, name="xs%d" % q) for q in range(TILES)]
         w1raw = const.tile([P, 8, 512], BF16)
         w2raw = const.tile([P, 4, 1024], BF16)
-        nc.scalar.dma_start(out=vecs[0:4, :], in_=fc1_b.rearrange("(r k) -> r k", r=4))
-        nc.scalar.dma_start(out=vecs[4:6, :], in_=fc2_b.rearrange("(r k) -> r k", r=2))
-        nc.scalar.dma_start(out=vecs[6:8, :], in_=mlp_norm_w.rearrange("(r k) -> r k", r=2))
-        nc.scalar.dma_start(out=vecs[8:10, :], in_=gamma_mlp.rearrange("(r k) -> r k", r=2))
 
-        def load_x(b, c0, c1):
+        def load_x(q):
+            c0 = (q % 4) * NT
             for u in range(2):
-                nc.sync.dma_start(out=xs[b][:, 2 * u:2 * u + 2, c0:c1], in_=xv[:, b, u, :, c0:c1])
+                nc.sync.dma_start(out=xs[q][:, 2 * u:2 * u + 2, :], in_=xv[:, q // 4, u, :, c0:c0 + NT])
 
         w1d = fc1_w.rearrange("(r m e) c -> m r (e c)", r=4, m=P, e=2)
         w1r = w1raw[:].rearrange("m (r e) c -> m r (e c)", e=2)
-        load_x(0, 0, NT)
         nc.sync.dma_start(out=w1r[:, 0:2, :], in_=w1d[:, 0:2, :])
+        load_x(0)
+        nc.sync.dma_start(out=vecs[0:4, :], in_=fc1_b.rearrange("(r k) -> r k", r=4))
+        nc.sync.dma_start(out=vecs[4:6, :], in_=fc2_b.rearrange("(r k) -> r k", r=2))
+        nc.sync.dma_start(out=vecs[6:8, :], in_=mlp_norm_w.rearrange("(r k) -> r k", r=2))
+        nc.sync.dma_start(out=vecs[8:10, :], in_=gamma_mlp.rearrange("(r k) -> r k", r=2))
         nc.sync.dma_start(out=w1r[:, 2:4, :], in_=w1d[:, 2:4, :])
-        load_x(0, NT, 2 * NT)
+        load_x(1)
+        load_x(2)
         nc.sync.dma_start(out=w2raw[:].rearrange("m (u e) f -> m u (e f)", e=2),
                           in_=fc2_w.rearrange("(u m e) f -> m u (e f)", u=2, m=P, e=2))
-        load_x(0, 2 * NT, NPOS)
-        load_x(1, 0, 2 * NT)
-        load_x(1, 2 * NT, NPOS)
-
-        pt = psa.tile([P, P], F32, tag="p1")
-        nc.tensor.transpose(pt[:], vecs[:].bitcast(F32), ident[:])
-        prw = const.tile([P, 16], F32)
-        nc.vector.tensor_copy(out=prw[:, 0:10], in_=pt[:, 0:10])
-        prm = const.tile([P, 20], F32)
-        nc.vector.tensor_copy(out=prm[:], in_=prw[:, 0:10].bitcast(BF16))
-        gw = const.tile([P, 4], F32)
-        nc.vector.tensor_tensor(out=gw[:], in0=prm[:, 12:16], in1=prm[:, 16:20], op=ALU.mult)
+        for q in range(3, TILES):
+            load_x(q)
 
         w1c = const.tile([P, 1024], U32, align_bytes=64)
         w1s = const.tile([P, 1024], U8, align_bytes=64)
-        w2c = const.tile([P, 2, 512], U32, align_bytes=64)
-        w2s = const.tile([P, 2, 512], U8, align_bytes=64)
+        w2c = const.tile([P, 4, 2, P], U32, align_bytes=64)
+        w2s = const.tile([P, 4, 2, P], U8, align_bytes=64)
         st = {}
 
         def x_regroup(q):
             xg = xgp.tile([P, NT, 4], BF16, align_bytes=64, name="xg")
-            regroup(nc, X_ENG[q], xg[:], xs[q // 4][:, :, (q % 4) * NT:(q % 4 + 1) * NT])
+            regroup(nc, X_ENG[q], xg[:], xs[q][:])
             st[("xg", q)] = xg
 
         def x_quant(q):
@@ -163,8 +155,7 @@ def tile_axialattentionblock_pc_t_kernel(tc, x2, fc1_w, fc1_b, fc2_w, fc2_b, mlp
             n = q % 4
             m2 = psb.tile([P, NT], F32, tag="m2", name="m2")
             for g in range(2):
-                nc.tensor.matmul_mx(out=m2[:], lhsT=w2c[:, g, P * i:P * i + P].bitcast(FP8X4),
-                                    lhsT_scale=w2s[:, g, P * i:P * i + P],
+                nc.tensor.matmul_mx(out=m2[:], lhsT=w2c[:, i, g, :].bitcast(FP8X4), lhsT_scale=w2s[:, i, g, :],
                                     rhs=hc[:, g, :].bitcast(FP8X4), rhs_scale=hsc[:, g, :],
                                     start=(g == 0), stop=(g == 1))
             if n == 0:
@@ -201,25 +192,25 @@ def tile_axialattentionblock_pc_t_kernel(tc, x2, fc1_w, fc1_b, fc2_w, fc2_b, mlp
             m = st[("m", b, i)]
             cs = slice(n * NT, (n + 1) * NT)
             nc.vector.scalar_tensor_tensor(out=m[:, cs], in0=m[:, cs], scalar=st[("av", b)][:, i:i + 1],
-                                           in1=xs[b][:, i, cs], op0=ALU.mult, op1=ALU.add)
+                                           in1=xs[4 * b + n][:, i, :], op0=ALU.mult, op1=ALU.add)
             if n % 2 == 1:
                 c2 = slice((n - 1) * NT, (n + 1) * NT)
                 nc.sync.dma_start(out=ov[:, b, i // 2, i % 2, c2], in_=m[:, c2])
 
         def w2_prep():
             w2g = const.tile([P, 4096], BF16, align_bytes=64, tag="wg", name="w2g")
-            w2g32 = w2g[:].bitcast(F32).rearrange("q (g i m u) -> q g i m u", g=2, i=4, m=P, u=2)
+            w2g32 = w2g[:].bitcast(F32).rearrange("q (i g m u) -> q i g m u", g=2, i=4, m=P, u=2)
             for i in range(4):
                 wt = psb.tile([P, 4, P], F32, tag="m2", name="wt2")
                 wsrc = w2raw[:, i, :].bitcast(F32)
                 for r in range(4):
                     nc.tensor.transpose(wt[:, r, :], wsrc[:, P * r:P * r + P], ident[:])
-                evac(nc, "SVSV"[i], w2g32[:, :, i, :, :], wt[:].rearrange("q (g u) m -> q g m u", g=2))
-            for g in range(2):
-                nc.vector.quantize_mx(out=w2c[:, g, :].bitcast(FP8X4), scales=w2s[:, g, :],
-                                      in_=w2g[:, 2048 * g:2048 * g + 2048])
+                evac(nc, "SVSV"[i], w2g32[:, i, :, :, :], wt[:].rearrange("q (g u) m -> q g m u", g=2))
+            for ip in range(2):
+                nc.vector.quantize_mx(out=w2c[:, 2 * ip:2 * ip + 2, :, :].rearrange("q i g m -> q (i g m)").bitcast(FP8X4),
+                                      scales=w2s[:, 2 * ip:2 * ip + 2, :, :].rearrange("q i g m -> q (i g m)"),
+                                      in_=w2g[:, 2048 * ip:2048 * ip + 2048])
 
-        x_regroup(0)
         w1g = const.tile([P, 4096], BF16, align_bytes=64, tag="wg", name="w1g")
         w1g32 = w1g[:].bitcast(F32).rearrange("q (j m u) -> q j m u", j=8, m=P, u=2)
         for jp in range(4):
@@ -233,11 +224,22 @@ def tile_axialattentionblock_pc_t_kernel(tc, x2, fc1_w, fc1_b, fc2_w, fc2_b, mlp
                     nc.tensor.transpose(wt[:, jj, u, :], wsrc[:, P * u:P * u + P], ident[:])
             evac(nc, "SSSV"[jp], w1g32[:, 2 * jp:2 * jp + 2, :, :], wt[:].rearrange("q j u m -> q j m u"))
             if jp == 0:
-                x_quant(0)
+                x_regroup(0)
             if jp % 2 == 1:
                 h0 = (jp // 2) * 512
                 nc.vector.quantize_mx(out=w1c[:, h0:h0 + 512].bitcast(FP8X4), scales=w1s[:, h0:h0 + 512],
                                       in_=w1g[:, 4 * h0:4 * h0 + 2048])
+            if jp == 1:
+                x_quant(0)
+                pt = psa.tile([P, P], F32, tag="p1")
+                nc.tensor.transpose(pt[:], vecs[:].bitcast(F32), ident[:])
+                prw = const.tile([P, 16], F32)
+                nc.vector.tensor_copy(out=prw[:, 0:10], in_=pt[:, 0:10])
+                prm = const.tile([P, 20], F32)
+                nc.vector.tensor_copy(out=prm[:], in_=prw[:, 0:10].bitcast(BF16))
+                gw = const.tile([P, 4], F32)
+                nc.vector.tensor_tensor(out=gw[:], in0=prm[:, 12:16], in1=prm[:, 16:20], op=ALU.mult)
+
 
         todo = []
 
@@ -246,11 +248,10 @@ def tile_axialattentionblock_pc_t_kernel(tc, x2, fc1_w, fc1_b, fc2_w, fc2_b, mlp
                 if todo:
                     final(*todo.pop(0))
 
-        for w in range(-4, HALVES + TAILW):
-            rate = FS if w < HALVES else FT
-            for q in range(1, TILES):
-                if 2 * q - LXR == w or (w == -4 and 2 * q - LXR < -4):
-                    x_regroup(q)
+        for w in range(2 - LXR, HALVES + TAILW):
+            k = w - LHR
+            if 0 <= k < HALVES and H_ENG[k] == "S":
+                h_regroup(k)
             if 0 <= w < HALVES:
                 mm1_gelu(w)
             if w == LW2:
@@ -259,22 +260,23 @@ def tile_axialattentionblock_pc_t_kernel(tc, x2, fc1_w, fc1_b, fc2_w, fc2_b, mlp
                 if w == 2 * q + 1 + LM2:
                     for i in range(4):
                         mm2_evac(q, i)
-            if 0 <= w - LHR < HALVES:
-                h_regroup(w - LHR)
             for q in range(1, TILES):
-                if 2 * q - LXQ == w or (w == -4 and 2 * q - LXQ < -4):
+                if 2 * q - LXQ == w:
                     x_quant(q)
-            finals(rate[0])
+            if 0 <= k < HALVES and H_ENG[k] != "S":
+                h_regroup(k)
+            for q in range(1, TILES):
+                if 2 * q - LXR == w:
+                    x_regroup(q)
             if 0 <= w - LHQ < HALVES:
                 h_quant(w - LHQ)
-            finals(rate[1])
             for q in range(TILES):
                 if w == 2 * q + 1 + LBN:
                     for i in range(4):
                         stats(q, i)
                     if q % 4 == 3:
                         chain1(q // 4)
-            finals(rate[2])
+            finals(2)
             for b in range(2):
                 if w == 2 * (4 * b + 3) + 1 + LBN + LC2:
                     chain2(b)

@@ -19,19 +19,18 @@ NT = 512
 TILES = 8
 HALVES = 2 * TILES
 
-X_ENG = "VVVVVVVV"
-H_ENG = "VVVSVVVSVVVSVVVS"
+H_SCALAR = (3, 11, 13, 15)
 LXR = 4
 LXQ = 2
 LW2 = 3
 LHR = 1
 LHQ = 2
 LM2 = 3
-LBN = 4
+LBN = (4, 3)
 LC2 = 1
-FS = (0, 0, 1)
-FT = (0, 0, 1)
-TAILW = 16
+VF0 = 16
+PF0 = 16
+PE_FINALS = ((2, 1), (3, 0), (3, 1))
 
 
 def regroup(nc, eng, dst, src):
@@ -39,10 +38,8 @@ def regroup(nc, eng, dst, src):
     s = src.rearrange("p t (c i) -> p c t i", i=4)
     if eng == "V":
         nc.vector.tensor_copy(out=d, in_=s)
-    elif eng == "S":
-        nc.scalar.copy(out=d, in_=s)
     else:
-        nc.gpsimd.tensor_scalar(out=d, in0=s, scalar1=1.0, scalar2=0.0, op0=ALU.mult, op1=ALU.add)
+        nc.scalar.copy(out=d, in_=s)
 
 
 def evac(nc, eng, dst, src):
@@ -61,8 +58,10 @@ def tile_axialattentionblock_pc_t_kernel(tc, x2, fc1_w, fc1_b, fc2_w, fc2_b, mlp
         xcp = ctx.enter_context(tc.tile_pool(name="xcp", bufs=3))
         hsp = ctx.enter_context(tc.tile_pool(name="hsp", bufs=4))
         hgp = ctx.enter_context(tc.tile_pool(name="hgp", bufs=4))
-        hcp = ctx.enter_context(tc.tile_pool(name="hcp", bufs=4))
-        msp = ctx.enter_context(tc.tile_pool(name="msp", bufs=8))
+        hcp = ctx.enter_context(tc.tile_pool(name="hcp", bufs=6))
+        msp = ctx.enter_context(tc.tile_pool(name="msp", bufs=4))
+        opl = ctx.enter_context(tc.tile_pool(name="opl", bufs=6))
+        xpp = ctx.enter_context(tc.tile_pool(name="xpp", bufs=4))
         sml = ctx.enter_context(tc.tile_pool(name="sml", bufs=2))
         psa = ctx.enter_context(tc.psum_pool(name="psa", bufs=4))
         psb = ctx.enter_context(tc.psum_pool(name="psb", bufs=4))
@@ -80,20 +79,25 @@ def tile_axialattentionblock_pc_t_kernel(tc, x2, fc1_w, fc1_b, fc2_w, fc2_b, mlp
         nc.vector.memset(half[:], 0.5)
         ident = const.tile([P, P], F32)
         make_identity(nc, ident[:])
+        identb = const.tile([P, P], BF16)
+        make_identity(nc, identb[:])
 
-        xs = [const.tile([P, 4, NT], BF16, name="xs%d" % q) for q in range(TILES)]
+        xp2 = [const.tile([P, 2, 4, NT], BF16, name="xp%d" % j) for j in range(TILES // 2)]
         w1raw = const.tile([P, 8, 512], BF16)
         w2raw = const.tile([P, 4, 1024], BF16)
+
+        def xs(q):
+            return xp2[q // 2][:, q % 2, :, :]
 
         def load_x(q):
             c0 = (q % 4) * NT
             for u in range(2):
-                nc.sync.dma_start(out=xs[q][:, 2 * u:2 * u + 2, :], in_=xv[:, q // 4, u, :, c0:c0 + NT])
+                nc.sync.dma_start(out=xs(q)[:, 2 * u:2 * u + 2, :], in_=xv[:, q // 4, u, :, c0:c0 + NT])
 
         w1d = fc1_w.rearrange("(r m e) c -> m r (e c)", r=4, m=P, e=2)
         w1r = w1raw[:].rearrange("m (r e) c -> m r (e c)", e=2)
-        nc.sync.dma_start(out=w1r[:, 0:2, :], in_=w1d[:, 0:2, :])
         load_x(0)
+        nc.sync.dma_start(out=w1r[:, 0:2, :], in_=w1d[:, 0:2, :])
         nc.sync.dma_start(out=vecs[0:4, :], in_=fc1_b.rearrange("(r k) -> r k", r=4))
         nc.sync.dma_start(out=vecs[4:6, :], in_=fc2_b.rearrange("(r k) -> r k", r=2))
         nc.sync.dma_start(out=vecs[6:8, :], in_=mlp_norm_w.rearrange("(r k) -> r k", r=2))
@@ -114,7 +118,7 @@ def tile_axialattentionblock_pc_t_kernel(tc, x2, fc1_w, fc1_b, fc2_w, fc2_b, mlp
 
         def x_regroup(q):
             xg = xgp.tile([P, NT, 4], BF16, align_bytes=64, name="xg")
-            regroup(nc, X_ENG[q], xg[:], xs[q][:])
+            regroup(nc, "V", xg[:], xs(q))
             st[("xg", q)] = xg
 
         def x_quant(q):
@@ -138,7 +142,7 @@ def tile_axialattentionblock_pc_t_kernel(tc, x2, fc1_w, fc1_b, fc2_w, fc2_b, mlp
 
         def h_regroup(k):
             hg = hgp.tile([P, NT, 4], BF16, align_bytes=64, name="hg")
-            regroup(nc, H_ENG[k], hg[:], st[("hs", k)][:])
+            regroup(nc, "S" if k in H_SCALAR else "V", hg[:], st[("hs", k)][:])
             st[("hg", k)] = hg
 
         def h_quant(k):
@@ -149,33 +153,47 @@ def tile_axialattentionblock_pc_t_kernel(tc, x2, fc1_w, fc1_b, fc2_w, fc2_b, mlp
             nc.vector.quantize_mx(out=hc[:, k % 2, :].bitcast(FP8X4), scales=hsc[:, k % 2, :],
                                   in_=st[("hg", k)][:].rearrange("p w t -> p (w t)"))
 
-        def mm2_evac(q, i):
+        def mm2(q, i, pool, tag):
             hc, hsc = st[("hc", q)]
-            b = q // 4
-            n = q % 4
-            m2 = psb.tile([P, NT], F32, tag="m2", name="m2")
+            m2 = pool.tile([P, NT], F32, tag=tag, name="m2")
             for g in range(2):
                 nc.tensor.matmul_mx(out=m2[:], lhsT=w2c[:, i, g, :].bitcast(FP8X4), lhsT_scale=w2s[:, i, g, :],
                                     rhs=hc[:, g, :].bitcast(FP8X4), rhs_scale=hsc[:, g, :],
                                     start=(g == 0), stop=(g == 1))
-            if n == 0:
-                st[("m", b, i)] = msp.tile([P, NPOS], F32, name="m")
-            nc.scalar.activation(out=st[("m", b, i)][:, n * NT:(n + 1) * NT], in_=m2[:], func=ACT.Identity,
-                                 bias=prm[:, 8 + i:9 + i], scale=1.0)
+            return m2
+
+        def mm2_first(q, i):
+            m2 = mm2(q, i, psb, "m2")
+            st[("p", q, i)] = m2
+            if q < 4:
+                if q == 0:
+                    st[("m", i)] = msp.tile([P, NPOS], F32, name="m")
+                nc.scalar.activation(out=st[("m", i)][:, q * NT:(q + 1) * NT], in_=m2[:], func=ACT.Identity,
+                                     bias=prm[:, 8 + i:9 + i], scale=1.0)
 
         def stats(q, i):
             b = q // 4
             n = q % 4
             if n == 0 and i == 0:
                 st[("bst", b)] = sml.tile([P, 4, 4, 6], F32, name="bst")
-            nc.vector.bn_stats(out=st[("bst", b)][:, i, n, :], in_=st[("m", b, i)][:, n * NT:(n + 1) * NT])
+            src = st[("m", i)][:, n * NT:(n + 1) * NT] if b == 0 else st[("p", q, i)][:]
+            nc.vector.bn_stats(out=st[("bst", b)][:, i, n, :], in_=src)
+
+        def evac_last(i):
+            o = opl.tile([P, 2 * NT], F32, tag="o", name="o")
+            st[("o", i, 1)] = o
+            nc.scalar.activation(out=o[:, NT:2 * NT], in_=st[("p", 7, i)][:], func=ACT.Identity,
+                                 bias=prm[:, 8 + i:9 + i], scale=1.0)
 
         def chain1(b):
             mv = sml.tile([P, 4, 2], F32, name="mv")
             for i in range(4):
                 nc.vector.bn_aggr(out=mv[:, i, :], in_=st[("bst", b)][:, i, :, :].rearrange("p n s -> p (n s)"))
             sd = sml.tile([P, 4], F32, name="sd")
-            nc.gpsimd.tensor_tensor(out=sd[:], in0=mv[:, :, 1], in1=half[:], op=ALU.pow)
+            if b == 0:
+                nc.gpsimd.tensor_tensor(out=sd[:], in0=mv[:, :, 1], in1=half[:], op=ALU.pow)
+            else:
+                nc.scalar.activation(out=sd[:], in_=mv[:, :, 1], func=ACT.Sqrt)
             st[("sd", b)] = sd
 
         def chain2(b):
@@ -187,15 +205,59 @@ def tile_axialattentionblock_pc_t_kernel(tc, x2, fc1_w, fc1_b, fc2_w, fc2_b, mlp
             av = sml.tile([P, 4], F32, name="av")
             nc.vector.tensor_tensor(out=av[:], in0=rc[:], in1=gw[:], op=ALU.mult)
             st[("av", b)] = av
+            if b == 1:
+                ab = sml.tile([P, 4], F32, name="ab")
+                nc.vector.tensor_tensor(out=ab[:], in0=av[:], in1=prm[:, 8:12], op=ALU.mult)
+                st["ab"] = ab
+            else:
+                for i in (2, 3):
+                    dg = const.tile([P, P], F32, name="dg%d" % i)
+                    nc.gpsimd.tensor_scalar_mul(dg[:], ident[:], av[:, i:i + 1])
+                    st[("dg", i)] = dg
 
-        def final(b, i, n):
-            m = st[("m", b, i)]
+        def final1_v(i, hf):
+            m = st[("m", i)]
+            c2 = slice(2 * hf * NT, 2 * (hf + 1) * NT)
+            mv = m[:, c2].rearrange("p (e n) -> p e n", e=2)
+            nc.vector.scalar_tensor_tensor(out=mv, in0=mv, scalar=st[("av", 0)][:, i:i + 1],
+                                           in1=xp2[hf][:, :, i, :], op0=ALU.mult, op1=ALU.add)
+            nc.sync.dma_start(out=ov[:, 0, i // 2, i % 2, c2], in_=m[:, c2])
+
+        def final1_p(i, hf, e):
+            m = st[("m", i)]
+            n = 2 * hf + e
             cs = slice(n * NT, (n + 1) * NT)
-            nc.vector.scalar_tensor_tensor(out=m[:, cs], in0=m[:, cs], scalar=st[("av", b)][:, i:i + 1],
-                                           in1=xs[4 * b + n][:, i, :], op0=ALU.mult, op1=ALU.add)
-            if n % 2 == 1:
-                c2 = slice((n - 1) * NT, (n + 1) * NT)
-                nc.sync.dma_start(out=ov[:, b, i // 2, i % 2, c2], in_=m[:, c2])
+            pf = psb.tile([P, NT], F32, tag="m2", name="pf")
+            nc.tensor.matmul(pf[:], lhsT=st[("dg", i)][:], rhs=m[:, cs], start=True, stop=False)
+            nc.tensor.matmul(pf[:], lhsT=identb[:], rhs=xs(n)[:, i, :], start=False, stop=True)
+            nc.scalar.copy(out=m[:, cs], in_=pf[:])
+            if e == 1:
+                c2 = slice(2 * hf * NT, 2 * (hf + 1) * NT)
+                nc.sync.dma_start(out=ov[:, 0, i // 2, i % 2, c2], in_=m[:, c2])
+
+        def final2(i, n, single):
+            q = 4 + n
+            hf = n // 2
+            av = st[("av", 1)]
+            if n == 3:
+                o = st[("o", i, 1)]
+                cs = slice(NT, 2 * NT)
+                nc.vector.scalar_tensor_tensor(out=o[:, cs], in0=o[:, cs], scalar=av[:, i:i + 1],
+                                               in1=xs(q)[:, i, :], op0=ALU.mult, op1=ALU.add)
+            else:
+                m2 = mm2(q, i, psa, "p1")
+                xb = xpp.tile([P, NT], F32, name="xb")
+                nc.scalar.activation(out=xb[:], in_=xs(q)[:, i, :], func=ACT.Identity, bias=st["ab"][:, i:i + 1], scale=1.0)
+                if n == 0:
+                    st[("o", i, 0)] = opl.tile([P, 2 * NT], F32, tag="o", name="o")
+                o = st[("o", i, hf)]
+                cs = slice((n % 2) * NT, (n % 2 + 1) * NT)
+                nc.vector.scalar_tensor_tensor(out=o[:, cs], in0=m2[:], scalar=av[:, i:i + 1], in1=xb[:],
+                                               op0=ALU.mult, op1=ALU.add)
+            if single:
+                nc.sync.dma_start(out=ov[:, 1, i // 2, i % 2, n * NT:(n + 1) * NT], in_=o[:, cs])
+            elif n in (1, 2):
+                nc.sync.dma_start(out=ov[:, 1, i // 2, i % 2, 2 * hf * NT:2 * (hf + 1) * NT], in_=o[:])
 
         def w2_prep():
             w2g = const.tile([P, 4096], BF16, align_bytes=64, tag="wg", name="w2g")
@@ -211,6 +273,8 @@ def tile_axialattentionblock_pc_t_kernel(tc, x2, fc1_w, fc1_b, fc2_w, fc2_b, mlp
                                       scales=w2s[:, 2 * ip:2 * ip + 2, :, :].rearrange("q i g m -> q (i g m)"),
                                       in_=w2g[:, 2048 * ip:2048 * ip + 2048])
 
+        x_regroup(0)
+        x_quant(0)
         w1g = const.tile([P, 4096], BF16, align_bytes=64, tag="wg", name="w1g")
         w1g32 = w1g[:].bitcast(F32).rearrange("q (j m u) -> q j m u", j=8, m=P, u=2)
         for jp in range(4):
@@ -222,15 +286,12 @@ def tile_axialattentionblock_pc_t_kernel(tc, x2, fc1_w, fc1_b, fc2_w, fc2_b, mlp
                 wsrc = w1raw[:, 2 * jp + jj, :].bitcast(F32)
                 for u in range(2):
                     nc.tensor.transpose(wt[:, jj, u, :], wsrc[:, P * u:P * u + P], ident[:])
-            evac(nc, "SSSV"[jp], w1g32[:, 2 * jp:2 * jp + 2, :, :], wt[:].rearrange("q j u m -> q j m u"))
-            if jp == 0:
-                x_regroup(0)
+            evac(nc, "SSSS"[jp], w1g32[:, 2 * jp:2 * jp + 2, :, :], wt[:].rearrange("q j u m -> q j m u"))
             if jp % 2 == 1:
                 h0 = (jp // 2) * 512
                 nc.vector.quantize_mx(out=w1c[:, h0:h0 + 512].bitcast(FP8X4), scales=w1s[:, h0:h0 + 512],
                                       in_=w1g[:, 4 * h0:4 * h0 + 2048])
             if jp == 1:
-                x_quant(0)
                 pt = psa.tile([P, P], F32, tag="p1")
                 nc.tensor.transpose(pt[:], vecs[:].bitcast(F32), ident[:])
                 prw = const.tile([P, 16], F32)
@@ -240,30 +301,27 @@ def tile_axialattentionblock_pc_t_kernel(tc, x2, fc1_w, fc1_b, fc2_w, fc2_b, mlp
                 gw = const.tile([P, 4], F32)
                 nc.vector.tensor_tensor(out=gw[:], in0=prm[:, 12:16], in1=prm[:, 16:20], op=ALU.mult)
 
-
-        todo = []
-
-        def finals(count):
-            for c in range(count):
-                if todo:
-                    final(*todo.pop(0))
-
-        for w in range(2 - LXR, HALVES + TAILW):
+        pieces = [(i, hf) for i in range(4) for hf in range(2)]
+        v_todo = [c for c in pieces if c not in PE_FINALS]
+        p_todo = [(i, hf, e) for i, hf in PE_FINALS for e in range(2)]
+        for w in range(2 - LXR, HALVES + LM2 + 2):
             k = w - LHR
-            if 0 <= k < HALVES and H_ENG[k] == "S":
+            if 0 <= k < HALVES and k in H_SCALAR:
                 h_regroup(k)
             if 0 <= w < HALVES:
                 mm1_gelu(w)
+            if w == HALVES:
+                nc.scalar.activation(out=warm[:], in_=zero1[:], func=ACT.Sqrt)
             if w == LW2:
                 w2_prep()
             for q in range(TILES):
                 if w == 2 * q + 1 + LM2:
                     for i in range(4):
-                        mm2_evac(q, i)
+                        mm2_first(q, i)
             for q in range(1, TILES):
                 if 2 * q - LXQ == w:
                     x_quant(q)
-            if 0 <= k < HALVES and H_ENG[k] != "S":
+            if 0 <= k < HALVES and k not in H_SCALAR:
                 h_regroup(k)
             for q in range(1, TILES):
                 if 2 * q - LXR == w:
@@ -271,14 +329,26 @@ def tile_axialattentionblock_pc_t_kernel(tc, x2, fc1_w, fc1_b, fc2_w, fc2_b, mlp
             if 0 <= w - LHQ < HALVES:
                 h_quant(w - LHQ)
             for q in range(TILES):
-                if w == 2 * q + 1 + LBN:
+                if w == 2 * q + 1 + LBN[q // 4]:
                     for i in range(4):
                         stats(q, i)
-                    if q % 4 == 3:
-                        chain1(q // 4)
-            finals(2)
-            for b in range(2):
-                if w == 2 * (4 * b + 3) + 1 + LBN + LC2:
-                    chain2(b)
-                    todo.extend([(b, i, n) for i in range(4) for n in range(4)])
-        finals(len(todo))
+                    if q == 3:
+                        chain1(0)
+                    if q == 7:
+                        for i in range(4):
+                            evac_last(i)
+            if w == 7 + LBN[0] + LC2:
+                chain2(0)
+            if w >= VF0 and v_todo:
+                final1_v(*v_todo.pop(0))
+            if w >= PF0 and p_todo:
+                final1_p(*p_todo.pop(0))
+        chain1(1)
+        chain2(1)
+        for c in v_todo:
+            final1_v(*c)
+        for c in p_todo:
+            final1_p(*c)
+        order = [(i, n) for i in range(4) for n in (3, 2, 0, 1)]
+        for i, n in order:
+            final2(i, n, (i, n) in order[-2:])

@@ -19,17 +19,18 @@ NT = 512
 TILES = 8
 HALVES = 2 * TILES
 
-H_SCALAR = (3, 11, 13, 15)
+H_SCALAR = (11, 13, 15)
+X_POOL = (4, 5, 6, 7)
 LXR = 4
 LXQ = 2
 LW2 = 3
 LHR = 1
 LHQ = 2
 LM2 = 3
-LBN = (4, 3)
+LBN = (3, 3)
 LC2 = 1
-VF0 = 16
-PF0 = 16
+VF0 = 13
+PF0 = 13
 PE_FINALS = ((2, 1), (3, 0), (3, 1))
 
 
@@ -75,6 +76,8 @@ def tile_axialattentionblock_pc_t_kernel(tc, x2, fc1_w, fc1_b, fc2_w, fc2_b, mlp
         nc.vector.memset(zero1[:], 0.0)
         warm = const.tile([P, 1], F32)
         nc.scalar.activation(out=warm[:], in_=zero1[:], func=ACT.Gelu)
+        ones1 = const.tile([P, 1], F32)
+        nc.vector.memset(ones1[:], 1.0)
         half = const.tile([P, 4], F32)
         nc.vector.memset(half[:], 0.5)
         ident = const.tile([P, P], F32)
@@ -119,6 +122,16 @@ def tile_axialattentionblock_pc_t_kernel(tc, x2, fc1_w, fc1_b, fc2_w, fc2_b, mlp
         def x_regroup(q):
             xg = xgp.tile([P, NT, 4], BF16, align_bytes=64, name="xg")
             regroup(nc, "V", xg[:], xs(q))
+            st[("xg", q)] = xg
+
+        def x_regroup_pool(q):
+            tick = sml.tile([P, 1], F32, name="tick")
+            nc.vector.memset(tick[:], 0.0)
+            xg = xgp.tile([P, NT, 4], BF16, align_bytes=64, name="xg")
+            for e in range(2):
+                cs = slice(256 * e, 256 * e + 256)
+                nc.gpsimd.tensor_scalar(out=xg[:, cs, :], in0=xs(q)[:, :, cs].rearrange("p t n -> p n t"),
+                                        scalar1=ones1[:], scalar2=tick[:], op0=ALU.mult, op1=ALU.add)
             st[("xg", q)] = xg
 
         def x_quant(q):
@@ -306,10 +319,10 @@ def tile_axialattentionblock_pc_t_kernel(tc, x2, fc1_w, fc1_b, fc2_w, fc2_b, mlp
         p_todo = [(i, hf, e) for i, hf in PE_FINALS for e in range(2)]
         for w in range(2 - LXR, HALVES + LM2 + 2):
             k = w - LHR
-            if 0 <= k < HALVES and k in H_SCALAR:
-                h_regroup(k)
             if 0 <= w < HALVES:
                 mm1_gelu(w)
+            if 0 <= k < HALVES and k in H_SCALAR:
+                h_regroup(k)
             if w == HALVES:
                 nc.scalar.activation(out=warm[:], in_=zero1[:], func=ACT.Sqrt)
             if w == LW2:
@@ -324,12 +337,14 @@ def tile_axialattentionblock_pc_t_kernel(tc, x2, fc1_w, fc1_b, fc2_w, fc2_b, mlp
             if 0 <= k < HALVES and k not in H_SCALAR:
                 h_regroup(k)
             for q in range(1, TILES):
-                if 2 * q - LXR == w:
+                if 2 * q - LXR == w and q not in X_POOL:
                     x_regroup(q)
             if 0 <= w - LHQ < HALVES:
                 h_quant(w - LHQ)
             for q in range(TILES):
                 if w == 2 * q + 1 + LBN[q // 4]:
+                    if q + 4 in X_POOL:
+                        x_regroup_pool(q + 4)
                     for i in range(4):
                         stats(q, i)
                     if q == 3:

@@ -21,6 +21,7 @@ HALVES = 2 * TILES
 
 H_SCALAR = (11, 13, 15)
 X_POOL = (4, 5, 6, 7)
+XSPLIT = 384
 LXR = 4
 LXQ = 2
 LW2 = 3
@@ -76,8 +77,6 @@ def tile_axialattentionblock_pc_t_kernel(tc, x2, fc1_w, fc1_b, fc2_w, fc2_b, mlp
         nc.vector.memset(zero1[:], 0.0)
         warm = const.tile([P, 1], F32)
         nc.scalar.activation(out=warm[:], in_=zero1[:], func=ACT.Gelu)
-        ones1 = const.tile([P, 1], F32)
-        nc.vector.memset(ones1[:], 1.0)
         half = const.tile([P, 4], F32)
         nc.vector.memset(half[:], 0.5)
         ident = const.tile([P, P], F32)
@@ -128,10 +127,11 @@ def tile_axialattentionblock_pc_t_kernel(tc, x2, fc1_w, fc1_b, fc2_w, fc2_b, mlp
             tick = sml.tile([P, 1], F32, name="tick")
             nc.vector.memset(tick[:], 0.0)
             xg = xgp.tile([P, NT, 4], BF16, align_bytes=64, name="xg")
-            for e in range(2):
-                cs = slice(256 * e, 256 * e + 256)
-                nc.gpsimd.tensor_scalar(out=xg[:, cs, :], in0=xs(q)[:, :, cs].rearrange("p t n -> p n t"),
-                                        scalar1=ones1[:], scalar2=tick[:], op0=ALU.mult, op1=ALU.add)
+            seen = sml.tile([P, 1], F32, name="seen")
+            nc.gpsimd.tensor_copy(out=seen[:], in_=tick[:])
+            cs = slice(0, XSPLIT)
+            nc.gpsimd.tensor_scalar(out=xg[:, cs, :], in0=xs(q)[:, :, cs].rearrange("p t n -> p n t"),
+                                    scalar1=1.0, scalar2=0.0, op0=ALU.mult, op1=ALU.add)
             st[("xg", q)] = xg
 
         def x_quant(q):
@@ -189,8 +189,7 @@ def tile_axialattentionblock_pc_t_kernel(tc, x2, fc1_w, fc1_b, fc2_w, fc2_b, mlp
             n = q % 4
             if n == 0 and i == 0:
                 st[("bst", b)] = sml.tile([P, 4, 4, 6], F32, name="bst")
-            src = st[("m", i)][:, n * NT:(n + 1) * NT] if b == 0 else st[("p", q, i)][:]
-            nc.vector.bn_stats(out=st[("bst", b)][:, i, n, :], in_=src)
+            nc.vector.bn_stats(out=st[("bst", b)][:, i, n, :], in_=st[("p", q, i)][:])
 
         def evac_last(i):
             o = opl.tile([P, 2 * NT], F32, tag="o", name="o")
@@ -347,6 +346,8 @@ def tile_axialattentionblock_pc_t_kernel(tc, x2, fc1_w, fc1_b, fc2_w, fc2_b, mlp
                         x_regroup_pool(q + 4)
                     for i in range(4):
                         stats(q, i)
+                    if q + 4 in X_POOL:
+                        regroup(nc, "V", st[("xg", q + 4)][:, XSPLIT:, :], xs(q + 4)[:, :, XSPLIT:])
                     if q == 3:
                         chain1(0)
                     if q == 7:

@@ -19,7 +19,7 @@ NT = 512
 TILES = 8
 HALVES = 2 * TILES
 
-H_SCALAR = (11, 13, 15)
+H_SCALAR = (3, 11, 13, 15)
 X_POOL = (4, 5, 6, 7)
 XSPLIT = 384
 LXR = 4
@@ -338,12 +338,13 @@ def tile_axialattentionblock_pc_t_kernel(tc, x2, fc1_w, fc1_b, fc2_w, fc2_b, mlp
             for q in range(1, TILES):
                 if 2 * q - LXR == w and q not in X_POOL:
                     x_regroup(q)
+            for q in X_POOL:
+                if w == 2 * (q - 4) + 1 + LBN[0]:
+                    x_regroup_pool(q)
             if 0 <= w - LHQ < HALVES:
                 h_quant(w - LHQ)
             for q in range(TILES):
                 if w == 2 * q + 1 + LBN[q // 4]:
-                    if q + 4 in X_POOL:
-                        x_regroup_pool(q + 4)
                     for i in range(4):
                         stats(q, i)
                     if q + 4 in X_POOL:

@@ -20,7 +20,7 @@ TILES = 8
 HALVES = 2 * TILES
 
 H_SCALAR = (3, 11, 13, 15)
-X_POOL = (4, 5, 6, 7)
+X_POOL = ()
 XSPLIT = 384
 LXR = 4
 LXQ = 2
@@ -98,13 +98,14 @@ def tile_axialattentionblock_pc_t_kernel(tc, x2, fc1_w, fc1_b, fc2_w, fc2_b, mlp
 
         w1d = fc1_w.rearrange("(r m e) c -> m r (e c)", r=4, m=P, e=2)
         w1r = w1raw[:].rearrange("m (r e) c -> m r (e c)", e=2)
-        load_x(0)
-        nc.sync.dma_start(out=w1r[:, 0:2, :], in_=w1d[:, 0:2, :])
+        nc.sync.dma_start(out=w1r[:, 0:1, :], in_=w1d[:, 0:1, :])
         nc.sync.dma_start(out=vecs[0:4, :], in_=fc1_b.rearrange("(r k) -> r k", r=4))
         nc.sync.dma_start(out=vecs[4:6, :], in_=fc2_b.rearrange("(r k) -> r k", r=2))
         nc.sync.dma_start(out=vecs[6:8, :], in_=mlp_norm_w.rearrange("(r k) -> r k", r=2))
         nc.sync.dma_start(out=vecs[8:10, :], in_=gamma_mlp.rearrange("(r k) -> r k", r=2))
-        nc.sync.dma_start(out=w1r[:, 2:4, :], in_=w1d[:, 2:4, :])
+        load_x(0)
+        for r in range(1, 4):
+            nc.sync.dma_start(out=w1r[:, r:r + 1, :], in_=w1d[:, r:r + 1, :])
         load_x(1)
         load_x(2)
         nc.sync.dma_start(out=w2raw[:].rearrange("m (u e) f -> m u (e f)", e=2),
@@ -285,33 +286,29 @@ def tile_axialattentionblock_pc_t_kernel(tc, x2, fc1_w, fc1_b, fc2_w, fc2_b, mlp
                                       scales=w2s[:, 2 * ip:2 * ip + 2, :, :].rearrange("q i g m -> q (i g m)"),
                                       in_=w2g[:, 2048 * ip:2048 * ip + 2048])
 
-        x_regroup(0)
-        x_quant(0)
         w1g = const.tile([P, 4096], BF16, align_bytes=64, tag="wg", name="w1g")
         w1g32 = w1g[:].bitcast(F32).rearrange("q (j m u) -> q j m u", j=8, m=P, u=2)
+        prw = const.tile([P, 16], F32)
+        prm = const.tile([P, 20], F32)
+        gw = const.tile([P, 4], F32)
         for jp in range(4):
-            if jp % 2 == 0:
-                wt = psa.tile([P, 2, 2, P], F32, tag="p1", name="wt1")
-            else:
-                wt = psb.tile([P, 2, 2, P], F32, tag="m2", name="wt1b")
+            wt = psa.tile([P, 2, 2, P], F32, tag="p1", name="wt1")
             for jj in range(2):
                 wsrc = w1raw[:, 2 * jp + jj, :].bitcast(F32)
                 for u in range(2):
                     nc.tensor.transpose(wt[:, jj, u, :], wsrc[:, P * u:P * u + P], ident[:])
-            evac(nc, "SSSS"[jp], w1g32[:, 2 * jp:2 * jp + 2, :, :], wt[:].rearrange("q j u m -> q j m u"))
-            if jp % 2 == 1:
-                h0 = (jp // 2) * 512
-                nc.vector.quantize_mx(out=w1c[:, h0:h0 + 512].bitcast(FP8X4), scales=w1s[:, h0:h0 + 512],
-                                      in_=w1g[:, 4 * h0:4 * h0 + 2048])
-            if jp == 1:
-                pt = psa.tile([P, P], F32, tag="p1")
+            nc.scalar.copy(out=w1g32[:, 2 * jp:2 * jp + 2, :, :], in_=wt[:].rearrange("q j u m -> q j m u"))
+            j0 = 256 * jp
+            nc.vector.quantize_mx(out=w1c[:, j0:j0 + 256].bitcast(FP8X4), scales=w1s[:, j0:j0 + 256],
+                                  in_=w1g[:, 4 * j0:4 * j0 + 1024])
+            if jp == 0:
+                pt = psb.tile([P, P], F32, tag="m2", name="pt")
                 nc.tensor.transpose(pt[:], vecs[:].bitcast(F32), ident[:])
-                prw = const.tile([P, 16], F32)
+                x_regroup(0)
                 nc.vector.tensor_copy(out=prw[:, 0:10], in_=pt[:, 0:10])
-                prm = const.tile([P, 20], F32)
+                x_quant(0)
                 nc.vector.tensor_copy(out=prm[:], in_=prw[:, 0:10].bitcast(BF16))
-                gw = const.tile([P, 4], F32)
-                nc.vector.tensor_tensor(out=gw[:], in0=prm[:, 12:16], in1=prm[:, 16:20], op=ALU.mult)
+        nc.vector.tensor_tensor(out=gw[:], in0=prm[:, 12:16], in1=prm[:, 16:20], op=ALU.mult)
 
         pieces = [(i, hf) for i in range(4) for hf in range(2)]
         v_todo = [c for c in pieces if c not in PE_FINALS]
@@ -352,15 +349,16 @@ def tile_axialattentionblock_pc_t_kernel(tc, x2, fc1_w, fc1_b, fc2_w, fc2_b, mlp
                     if q == 3:
                         chain1(0)
                     if q == 7:
-                        for i in range(4):
+                        for i in range(3):
                             evac_last(i)
+                        chain1(1)
+                        evac_last(3)
             if w == 7 + LBN[0] + LC2:
                 chain2(0)
             if w >= VF0 and v_todo:
                 final1_v(*v_todo.pop(0))
             if w >= PF0 and p_todo:
                 final1_p(*p_todo.pop(0))
-        chain1(1)
         chain2(1)
         for c in v_todo:
             final1_v(*c)
@@ -368,4 +366,4 @@ def tile_axialattentionblock_pc_t_kernel(tc, x2, fc1_w, fc1_b, fc2_w, fc2_b, mlp
             final1_p(*c)
         order = [(i, n) for i in range(4) for n in (3, 2, 0, 1)]
         for i, n in order:
-            final2(i, n, (i, n) in order[-2:])
+            final2(i, n, (i, n) in order[:2] + order[-2:])

@@ -28,10 +28,10 @@ LW2 = 3
 LHR = 1
 LHQ = 2
 LM2 = 3
-LBN = (3, 3)
+LBN = (4, 3)
 LC2 = 1
-VF0 = 13
-PF0 = 13
+VF0 = 14
+PF0 = 14
 PE_FINALS = ((2, 1), (3, 0), (3, 1))
 
 
@@ -190,7 +190,8 @@ def tile_axialattentionblock_pc_t_kernel(tc, x2, fc1_w, fc1_b, fc2_w, fc2_b, mlp
             n = q % 4
             if n == 0 and i == 0:
                 st[("bst", b)] = sml.tile([P, 4, 4, 6], F32, name="bst")
-            nc.vector.bn_stats(out=st[("bst", b)][:, i, n, :], in_=st[("p", q, i)][:])
+            src = st[("m", i)][:, n * NT:(n + 1) * NT] if b == 0 else st[("p", q, i)][:]
+            nc.vector.bn_stats(out=st[("bst", b)][:, i, n, :], in_=src)
 
         def evac_last(i):
             o = opl.tile([P, 2 * NT], F32, tag="o", name="o")

@@ -29,10 +29,11 @@ LHR = 1
 LHQ = 2
 LM2 = 3
 LBN = (4, 3)
-LC2 = 1
+UNBIASED = (NPOS / (NPOS - 1.0)) ** 0.5
 VF0 = 14
 PF0 = 14
 PE_FINALS = ((2, 1), (3, 0), (3, 1))
+V_LAST = (2, 0)
 
 
 def regroup(nc, eng, dst, src):
@@ -79,6 +80,8 @@ def tile_axialattentionblock_pc_t_kernel(tc, x2, fc1_w, fc1_b, fc2_w, fc2_b, mlp
         nc.scalar.activation(out=warm[:], in_=zero1[:], func=ACT.Gelu)
         half = const.tile([P, 4], F32)
         nc.vector.memset(half[:], 0.5)
+        neg1 = const.tile([P, 4], F32)
+        nc.vector.memset(neg1[:], -1.0)
         ident = const.tile([P, P], F32)
         make_identity(nc, ident[:])
         identb = const.tile([P, P], BF16)
@@ -199,43 +202,55 @@ def tile_axialattentionblock_pc_t_kernel(tc, x2, fc1_w, fc1_b, fc2_w, fc2_b, mlp
             nc.scalar.activation(out=o[:, NT:2 * NT], in_=st[("p", 7, i)][:], func=ACT.Identity,
                                  bias=prm[:, 8 + i:9 + i], scale=1.0)
 
-        def chain1(b):
+        def variances(b):
             mv = sml.tile([P, 4, 2], F32, name="mv")
             for i in range(4):
                 nc.vector.bn_aggr(out=mv[:, i, :], in_=st[("bst", b)][:, i, :, :].rearrange("p n s -> p (n s)"))
-            sd = sml.tile([P, 4], F32, name="sd")
-            if b == 0:
-                nc.gpsimd.tensor_tensor(out=sd[:], in0=mv[:, :, 1], in1=half[:], op=ALU.pow)
-            else:
-                nc.scalar.activation(out=sd[:], in_=mv[:, :, 1], func=ACT.Sqrt)
-            st[("sd", b)] = sd
+            return mv
 
-        def chain2(b):
+        def factors1():
+            mv = variances(0)
+            sd = sml.tile([P, 4], F32, name="sd")
+            nc.gpsimd.tensor_tensor(out=sd[:], in0=mv[:, :, 1], in1=half[:], op=ALU.pow)
             se = sml.tile([P, 4], F32, name="se")
-            nc.vector.tensor_scalar(out=se[:], in0=st[("sd", b)][:], scalar1=(NPOS / (NPOS - 1.0)) ** 0.5, scalar2=1e-8,
-                                    op0=ALU.mult, op1=ALU.add)
+            nc.gpsimd.tensor_scalar(out=se[:], in0=sd[:], scalar1=UNBIASED, scalar2=1e-8, op0=ALU.mult, op1=ALU.add)
+            rc = sml.tile([P, 4], F32, name="rc")
+            nc.gpsimd.tensor_tensor(out=rc[:], in0=se[:], in1=neg1[:], op=ALU.pow)
+            av = sml.tile([P, 4], F32, name="av")
+            nc.gpsimd.tensor_tensor(out=av[:], in0=rc[:], in1=gw[:], op=ALU.mult)
+            st[("av", 0)] = av
+            for i in (2, 3):
+                dg = const.tile([P, P], F32, name="dg%d" % i)
+                nc.gpsimd.tensor_scalar(out=dg[:], in0=ident[:], scalar1=av[:, i:i + 1], scalar2=zero1[:], op0=ALU.mult, op1=ALU.add)
+                st[("dg", i)] = dg
+
+        def root2():
+            mv = variances(1)
+            sd = sml.tile([P, 4], F32, name="sd")
+            nc.scalar.activation(out=sd[:], in_=mv[:, :, 1], func=ACT.Sqrt)
+            st["sd"] = sd
+
+        def factors2():
+            se = sml.tile([P, 4], F32, name="se")
+            nc.vector.tensor_scalar(out=se[:], in0=st["sd"][:], scalar1=UNBIASED, scalar2=1e-8, op0=ALU.mult, op1=ALU.add)
             rc = sml.tile([P, 4], F32, name="rc")
             nc.vector.reciprocal(out=rc[:], in_=se[:])
             av = sml.tile([P, 4], F32, name="av")
             nc.vector.tensor_tensor(out=av[:], in0=rc[:], in1=gw[:], op=ALU.mult)
-            st[("av", b)] = av
-            if b == 1:
-                ab = sml.tile([P, 4], F32, name="ab")
-                nc.vector.tensor_tensor(out=ab[:], in0=av[:], in1=prm[:, 8:12], op=ALU.mult)
-                st["ab"] = ab
-            else:
-                for i in (2, 3):
-                    dg = const.tile([P, P], F32, name="dg%d" % i)
-                    nc.gpsimd.tensor_scalar_mul(dg[:], ident[:], av[:, i:i + 1])
-                    st[("dg", i)] = dg
+            st[("av", 1)] = av
+            ab = sml.tile([P, 4], F32, name="ab")
+            nc.vector.tensor_tensor(out=ab[:], in0=av[:], in1=prm[:, 8:12], op=ALU.mult)
+            st["ab"] = ab
 
         def final1_v(i, hf):
             m = st[("m", i)]
-            c2 = slice(2 * hf * NT, 2 * (hf + 1) * NT)
-            mv = m[:, c2].rearrange("p (e n) -> p e n", e=2)
-            nc.vector.scalar_tensor_tensor(out=mv, in0=mv, scalar=st[("av", 0)][:, i:i + 1],
-                                           in1=xp2[hf][:, :, i, :], op0=ALU.mult, op1=ALU.add)
-            nc.sync.dma_start(out=ov[:, 0, i // 2, i % 2, c2], in_=m[:, c2])
+            width = 1 if (i, hf) == V_LAST else 2
+            for n in range(2 * hf, 2 * hf + 2, width):
+                cs = slice(n * NT, (n + width) * NT)
+                mv = m[:, cs].rearrange("p (e n) -> p e n", e=width)
+                nc.vector.scalar_tensor_tensor(out=mv, in0=mv, scalar=st[("av", 0)][:, i:i + 1],
+                                               in1=xp2[hf][:, n - 2 * hf:n - 2 * hf + width, i, :], op0=ALU.mult, op1=ALU.add)
+                nc.sync.dma_start(out=ov[:, 0, i // 2, i % 2, cs], in_=m[:, cs])
 
         def final1_p(i, hf, e):
             m = st[("m", i)]
@@ -306,10 +321,10 @@ def tile_axialattentionblock_pc_t_kernel(tc, x2, fc1_w, fc1_b, fc2_w, fc2_b, mlp
                 pt = psb.tile([P, P], F32, tag="m2", name="pt")
                 nc.tensor.transpose(pt[:], vecs[:].bitcast(F32), ident[:])
                 x_regroup(0)
-                nc.vector.tensor_copy(out=prw[:, 0:10], in_=pt[:, 0:10])
+                nc.scalar.copy(out=prw[:, 0:10], in_=pt[:, 0:10])
                 x_quant(0)
-                nc.vector.tensor_copy(out=prm[:], in_=prw[:, 0:10].bitcast(BF16))
-        nc.vector.tensor_tensor(out=gw[:], in0=prm[:, 12:16], in1=prm[:, 16:20], op=ALU.mult)
+                nc.scalar.copy(out=prm[:], in_=prw[:, 0:10].bitcast(BF16))
+        nc.gpsimd.tensor_tensor(out=gw[:], in0=prm[:, 12:16], in1=prm[:, 16:20], op=ALU.mult)
 
         pieces = [(i, hf) for i in range(4) for hf in range(2)]
         v_todo = [c for c in pieces if c not in PE_FINALS]
@@ -343,24 +358,22 @@ def tile_axialattentionblock_pc_t_kernel(tc, x2, fc1_w, fc1_b, fc2_w, fc2_b, mlp
                 h_quant(w - LHQ)
             for q in range(TILES):
                 if w == 2 * q + 1 + LBN[q // 4]:
+                    if q == 4:
+                        factors1()
                     for i in range(4):
                         stats(q, i)
                     if q + 4 in X_POOL:
                         regroup(nc, "V", st[("xg", q + 4)][:, XSPLIT:, :], xs(q + 4)[:, :, XSPLIT:])
-                    if q == 3:
-                        chain1(0)
                     if q == 7:
                         for i in range(3):
                             evac_last(i)
-                        chain1(1)
+                        root2()
                         evac_last(3)
-            if w == 7 + LBN[0] + LC2:
-                chain2(0)
             if w >= VF0 and v_todo:
                 final1_v(*v_todo.pop(0))
             if w >= PF0 and p_todo:
                 final1_p(*p_todo.pop(0))
-        chain2(1)
+        factors2()
         for c in v_todo:
             final1_v(*c)
         for c in p_todo:

@@ -101,12 +101,12 @@ def tile_axialattentionblock_pc_t_kernel(tc, x2, fc1_w, fc1_b, fc2_w, fc2_b, mlp
 
         w1d = fc1_w.rearrange("(r m e) c -> m r (e c)", r=4, m=P, e=2)
         w1r = w1raw[:].rearrange("m (r e) c -> m r (e c)", e=2)
+        load_x(0)
         nc.sync.dma_start(out=w1r[:, 0:1, :], in_=w1d[:, 0:1, :])
         nc.sync.dma_start(out=vecs[0:4, :], in_=fc1_b.rearrange("(r k) -> r k", r=4))
         nc.sync.dma_start(out=vecs[4:6, :], in_=fc2_b.rearrange("(r k) -> r k", r=2))
         nc.sync.dma_start(out=vecs[6:8, :], in_=mlp_norm_w.rearrange("(r k) -> r k", r=2))
         nc.sync.dma_start(out=vecs[8:10, :], in_=gamma_mlp.rearrange("(r k) -> r k", r=2))
-        load_x(0)
         for r in range(1, 4):
             nc.sync.dma_start(out=w1r[:, r:r + 1, :], in_=w1d[:, r:r + 1, :])
         load_x(1)
@@ -307,6 +307,8 @@ def tile_axialattentionblock_pc_t_kernel(tc, x2, fc1_w, fc1_b, fc2_w, fc2_b, mlp
         prw = const.tile([P, 16], F32)
         prm = const.tile([P, 20], F32)
         gw = const.tile([P, 4], F32)
+        x_regroup(0)
+        x_quant(0)
         for jp in range(4):
             wt = psa.tile([P, 2, 2, P], F32, tag="p1", name="wt1")
             for jj in range(2):
@@ -320,9 +322,7 @@ def tile_axialattentionblock_pc_t_kernel(tc, x2, fc1_w, fc1_b, fc2_w, fc2_b, mlp
             if jp == 0:
                 pt = psb.tile([P, P], F32, tag="m2", name="pt")
                 nc.tensor.transpose(pt[:], vecs[:].bitcast(F32), ident[:])
-                x_regroup(0)
                 nc.scalar.copy(out=prw[:, 0:10], in_=pt[:, 0:10])
-                x_quant(0)
                 nc.scalar.copy(out=prm[:], in_=prw[:, 0:10].bitcast(BF16))
         nc.gpsimd.tensor_tensor(out=gw[:], in0=prm[:, 12:16], in1=prm[:, 16:20], op=ALU.mult)
 

from contextlib import ExitStack

import concourse.mybir as mybir
from concourse.masks import make_identity

F32 = mybir.dt.float32
BF16 = mybir.dt.bfloat16
U32 = mybir.dt.uint32
U8 = mybir.dt.uint8
FP8X4 = mybir.dt.float8_e4m3fn_x4
ACT = mybir.ActivationFunctionType
ALU = mybir.AluOpType

FLOPS = 2 * 4096 * 512 * 1024 * 2

P = 128
NPOS = 2048
NT = 512
TILES = 8
HALVES = 2 * TILES

H_SCALAR = (3, 11, 13, 15)
X_POOL = ()
XSPLIT = 384
LXR = 4
LXQ = 2
LW2 = 3
LHR = 1
LHQ = 2
LM2 = 3
LBN = (4, 3)
UNBIASED = (NPOS / (NPOS - 1.0)) ** 0.5
VF0 = 14
PF0 = 14
PE_FINALS = ((2, 1), (3, 0), (3, 1))
V_LAST = (2, 0)


def regroup(nc, eng, dst, src):
    d = dst.rearrange("p (c i) t -> p c t i", i=4)
    s = src.rearrange("p t (c i) -> p c t i", i=4)
    if eng == "V":
        nc.vector.tensor_copy(out=d, in_=s)
    else:
        nc.scalar.copy(out=d, in_=s)


def evac(nc, eng, dst, src):
    if eng == "V":
        nc.vector.tensor_copy(out=dst, in_=src)
    else:
        nc.scalar.copy(out=dst, in_=src)


def tile_axialattentionblock_pc_t_kernel(tc, x2, fc1_w, fc1_b, fc2_w, fc2_b, mlp_norm_w, gamma_mlp, out):
    nc = tc.nc
    with ExitStack() as ctx:
        ctx.enter_context(tc.manual_schedule())
        const = ctx.enter_context(tc.tile_pool(name="const", bufs=1))
        xgp = ctx.enter_context(tc.tile_pool(name="xgp", bufs=3))
        xcp = ctx.enter_context(tc.tile_pool(name="xcp", bufs=3))
        hsp = ctx.enter_context(tc.tile_pool(name="hsp", bufs=4))
        hgp = ctx.enter_context(tc.tile_pool(name="hgp", bufs=4))
        hcp = ctx.enter_context(tc.tile_pool(name="hcp", bufs=6))
        msp = ctx.enter_context(tc.tile_pool(name="msp", bufs=4))
        opl = ctx.enter_context(tc.tile_pool(name="opl", bufs=6))
        xpp = ctx.enter_context(tc.tile_pool(name="xpp", bufs=4))
        sml = ctx.enter_context(tc.tile_pool(name="sml", bufs=2))
        psa = ctx.enter_context(tc.psum_pool(name="psa", bufs=4))
        psb = ctx.enter_context(tc.psum_pool(name="psb", bufs=4))

        xv = x2.rearrange("b (u q e) h w -> q b u e (h w)", u=2, q=P, e=2)
        ov = out.rearrange("b (u q e) h w -> q b u e (h w)", u=2, q=P, e=2)

        vecs = const.tile([P, 256], BF16)
        nc.vector.memset(vecs[:], 0.0)
        zero1 = const.tile([P, 1], F32)
        nc.vector.memset(zero1[:], 0.0)
        warm = const.tile([P, 1], F32)
        nc.scalar.activation(out=warm[:], in_=zero1[:], func=ACT.Gelu)
        half = const.tile([P, 4], F32)
        nc.vector.memset(half[:], 0.5)
        neg1 = const.tile([P, 4], F32)
        nc.vector.memset(neg1[:], -1.0)
        ident = const.tile([P, P], F32)
        make_identity(nc, ident[:])
        identb = const.tile([P, P], BF16)
        make_identity(nc, identb[:])

        xp2 = [const.tile([P, 2, 4, NT], BF16, name="xp%d" % j) for j in range(TILES // 2)]
        w1raw = const.tile([P, 8, 512], BF16)
        w2raw = const.tile([P, 4, 1024], BF16)

        def xs(q):
            return xp2[q // 2][:, q % 2, :, :]

        def load_x(q):
            c0 = (q % 4) * NT
            for u in range(2):
                nc.sync.dma_start(out=xs(q)[:, 2 * u:2 * u + 2, :], in_=xv[:, q // 4, u, :, c0:c0 + NT])

        w1d = fc1_w.rearrange("(r m e) c -> m r (e c)", r=4, m=P, e=2)
        w1r = w1raw[:].rearrange("m (r e) c -> m r (e c)", e=2)
        load_x(0)
        nc.sync.dma_start(out=w1r[:, 0:1, :], in_=w1d[:, 0:1, :])
        nc.sync.dma_start(out=vecs[0:4, :], in_=fc1_b.rearrange("(r k) -> r k", r=4))
        nc.sync.dma_start(out=vecs[4:6, :], in_=fc2_b.rearrange("(r k) -> r k", r=2))
        nc.sync.dma_start(out=vecs[6:8, :], in_=mlp_norm_w.rearrange("(r k) -> r k", r=2))
        nc.sync.dma_start(out=vecs[8:10, :], in_=gamma_mlp.rearrange("(r k) -> r k", r=2))
        for r in range(1, 4):
            nc.sync.dma_start(out=w1r[:, r:r + 1, :], in_=w1d[:, r:r + 1, :])
        load_x(1)
        load_x(2)
        nc.sync.dma_start(out=w2raw[:].rearrange("m (u e) f -> m u (e f)", e=2),
                          in_=fc2_w.rearrange("(u m e) f -> m u (e f)", u=2, m=P, e=2))
        for q in range(3, TILES):
            load_x(q)

        w1c = const.tile([P, 1024], U32, align_bytes=64)
        w1s = const.tile([P, 1024], U8, align_bytes=64)
        w2c = const.tile([P, 4, 2, P], U32, align_bytes=64)
        w2s = const.tile([P, 4, 2, P], U8, align_bytes=64)
        st = {}

        def x_regroup(q):
            xg = xgp.tile([P, NT, 4], BF16, align_bytes=64, name="xg")
            regroup(nc, "V", xg[:], xs(q))
            st[("xg", q)] = xg

        def x_regroup_pool(q):
            tick = sml.tile([P, 1], F32, name="tick")
            nc.vector.memset(tick[:], 0.0)
            xg = xgp.tile([P, NT, 4], BF16, align_bytes=64, name="xg")
            seen = sml.tile([P, 1], F32, name="seen")
            nc.gpsimd.tensor_copy(out=seen[:], in_=tick[:])
            cs = slice(0, XSPLIT)
            nc.gpsimd.tensor_scalar(out=xg[:, cs, :], in0=xs(q)[:, :, cs].rearrange("p t n -> p n t"),
                                    scalar1=1.0, scalar2=0.0, op0=ALU.mult, op1=ALU.add)
            st[("xg", q)] = xg

        def x_quant(q):
            xc = xcp.tile([P, NT], U32, align_bytes=64, name="xc")
            xsc = xcp.tile([P, NT], U8, align_bytes=64, name="xsc")
            nc.vector.quantize_mx(out=xc[:].bitcast(FP8X4), scales=xsc[:], in_=st[("xg", q)][:].rearrange("p w t -> p (w t)"))
            st[("xc", q)] = (xc, xsc)

        def mm1_gelu(k):
            xc, xsc = st[("xc", k // 2)]
            g = k % 2
            hs = hsp.tile([P, 4, NT], BF16, name="hs")
            for t in range(4):
                j = 4 * g + t
                p1 = psa.tile([P, NT], F32, tag="p1", name="p1")
                nc.tensor.matmul_mx(out=p1[:], lhsT=w1c[:, P * j:P * j + P].bitcast(FP8X4),
                                    lhsT_scale=w1s[:, P * j:P * j + P],
                                    rhs=xc[:].bitcast(FP8X4), rhs_scale=xsc[:], start=True, stop=True)
                nc.scalar.activation(out=hs[:, t, :], in_=p1[:], func=ACT.Gelu, bias=prm[:, j:j + 1], scale=1.0)
            st[("hs", k)] = hs

        def h_regroup(k):
            hg = hgp.tile([P, NT, 4], BF16, align_bytes=64, name="hg")
            regroup(nc, "S" if k in H_SCALAR else "V", hg[:], st[("hs", k)][:])
            st[("hg", k)] = hg

        def h_quant(k):
            if k % 2 == 0:
                st[("hc", k // 2)] = (hcp.tile([P, 2, NT], U32, align_bytes=64, name="hc"),
                                      hcp.tile([P, 2, NT], U8, align_bytes=64, name="hsc"))
            hc, hsc = st[("hc", k // 2)]
            nc.vector.quantize_mx(out=hc[:, k % 2, :].bitcast(FP8X4), scales=hsc[:, k % 2, :],
                                  in_=st[("hg", k)][:].rearrange("p w t -> p (w t)"))

        def mm2(q, i, pool, tag):
            hc, hsc = st[("hc", q)]
            m2 = pool.tile([P, NT], F32, tag=tag, name="m2")
            for g in range(2):
                nc.tensor.matmul_mx(out=m2[:], lhsT=w2c[:, i, g, :].bitcast(FP8X4), lhsT_scale=w2s[:, i, g, :],
                                    rhs=hc[:, g, :].bitcast(FP8X4), rhs_scale=hsc[:, g, :],
                                    start=(g == 0), stop=(g == 1))
            return m2

        def mm2_first(q, i):
            m2 = mm2(q, i, psb, "m2")
            st[("p", q, i)] = m2
            if q < 4:
                if q == 0:
                    st[("m", i)] = msp.tile([P, NPOS], F32, name="m")
                nc.scalar.activation(out=st[("m", i)][:, q * NT:(q + 1) * NT], in_=m2[:], func=ACT.Identity,
                                     bias=prm[:, 8 + i:9 + i], scale=1.0)

        def stats(q, i):
            b = q // 4
            n = q % 4
            if n == 0 and i == 0:
                st[("bst", b)] = sml.tile([P, 4, 4, 6], F32, name="bst")
            src = st[("m", i)][:, n * NT:(n + 1) * NT] if b == 0 else st[("p", q, i)][:]
            nc.vector.bn_stats(out=st[("bst", b)][:, i, n, :], in_=src)

        def evac_last(i):
            o = opl.tile([P, 2 * NT], F32, tag="o", name="o")
            st[("o", i, 1)] = o
            nc.scalar.activation(out=o[:, NT:2 * NT], in_=st[("p", 7, i)][:], func=ACT.Identity,
                                 bias=prm[:, 8 + i:9 + i], scale=1.0)

        def variances(b):
            mv = sml.tile([P, 4, 2], F32, name="mv")
            for i in range(4):
                nc.vector.bn_aggr(out=mv[:, i, :], in_=st[("bst", b)][:, i, :, :].rearrange("p n s -> p (n s)"))
            return mv

        def factors1():
            mv = variances(0)
            sd = sml.tile([P, 4], F32, name="sd")
            nc.gpsimd.tensor_tensor(out=sd[:], in0=mv[:, :, 1], in1=half[:], op=ALU.pow)
            se = sml.tile([P, 4], F32, name="se")
            nc.gpsimd.tensor_scalar(out=se[:], in0=sd[:], scalar1=UNBIASED, scalar2=1e-8, op0=ALU.mult, op1=ALU.add)
            rc = sml.tile([P, 4], F32, name="rc")
            nc.gpsimd.tensor_tensor(out=rc[:], in0=se[:], in1=neg1[:], op=ALU.pow)
            av = sml.tile([P, 4], F32, name="av")
            nc.gpsimd.tensor_tensor(out=av[:], in0=rc[:], in1=gw[:], op=ALU.mult)
            st[("av", 0)] = av
            for i in (2, 3):
                dg = const.tile([P, P], F32, name="dg%d" % i)
                nc.gpsimd.tensor_scalar(out=dg[:], in0=ident[:], scalar1=av[:, i:i + 1], scalar2=zero1[:], op0=ALU.mult, op1=ALU.add)
                st[("dg", i)] = dg

        def root2():
            mv = variances(1)
            sd = sml.tile([P, 4], F32, name="sd")
            nc.scalar.activation(out=sd[:], in_=mv[:, :, 1], func=ACT.Sqrt)
            st["sd"] = sd

        def factors2():
            se = sml.tile([P, 4], F32, name="se")
            nc.vector.tensor_scalar(out=se[:], in0=st["sd"][:], scalar1=UNBIASED, scalar2=1e-8, op0=ALU.mult, op1=ALU.add)
            rc = sml.tile([P, 4], F32, name="rc")
            nc.vector.reciprocal(out=rc[:], in_=se[:])
            av = sml.tile([P, 4], F32, name="av")
            nc.vector.tensor_tensor(out=av[:], in0=rc[:], in1=gw[:], op=ALU.mult)
            st[("av", 1)] = av
            ab = sml.tile([P, 4], F32, name="ab")
            nc.vector.tensor_tensor(out=ab[:], in0=av[:], in1=prm[:, 8:12], op=ALU.mult)
            st["ab"] = ab

        def final1_v(i, hf):
            m = st[("m", i)]
            width = 1 if (i, hf) == V_LAST else 2
            for n in range(2 * hf, 2 * hf + 2, width):
                cs = slice(n * NT, (n + width) * NT)
                mv = m[:, cs].rearrange("p (e n) -> p e n", e=width)
                nc.vector.scalar_tensor_tensor(out=mv, in0=mv, scalar=st[("av", 0)][:, i:i + 1],
                                               in1=xp2[hf][:, n - 2 * hf:n - 2 * hf + width, i, :], op0=ALU.mult, op1=ALU.add)
                nc.sync.dma_start(out=ov[:, 0, i // 2, i % 2, cs], in_=m[:, cs])

        def final1_p(i, hf, e):
            m = st[("m", i)]
            n = 2 * hf + e
            cs = slice(n * NT, (n + 1) * NT)
            pf = psb.tile([P, NT], F32, tag="m2", name="pf")
            nc.tensor.matmul(pf[:], lhsT=st[("dg", i)][:], rhs=m[:, cs], start=True, stop=False)
            nc.tensor.matmul(pf[:], lhsT=identb[:], rhs=xs(n)[:, i, :], start=False, stop=True)
            nc.scalar.copy(out=m[:, cs], in_=pf[:])
            if e == 1:
                c2 = slice(2 * hf * NT, 2 * (hf + 1) * NT)
                nc.sync.dma_start(out=ov[:, 0, i // 2, i % 2, c2], in_=m[:, c2])

        def final2(i, n, single):
            q = 4 + n
            hf = n // 2
            av = st[("av", 1)]
            if n == 3:
                o = st[("o", i, 1)]
                cs = slice(NT, 2 * NT)
                nc.vector.scalar_tensor_tensor(out=o[:, cs], in0=o[:, cs], scalar=av[:, i:i + 1],
                                               in1=xs(q)[:, i, :], op0=ALU.mult, op1=ALU.add)
            else:
                m2 = mm2(q, i, psa, "p1")
                xb = xpp.tile([P, NT], F32, name="xb")
                nc.scalar.activation(out=xb[:], in_=xs(q)[:, i, :], func=ACT.Identity, bias=st["ab"][:, i:i + 1], scale=1.0)
                if n == 0:
                    st[("o", i, 0)] = opl.tile([P, 2 * NT], F32, tag="o", name="o")
                o = st[("o", i, hf)]
                cs = slice((n % 2) * NT, (n % 2 + 1) * NT)
                nc.vector.scalar_tensor_tensor(out=o[:, cs], in0=m2[:], scalar=av[:, i:i + 1], in1=xb[:],
                                               op0=ALU.mult, op1=ALU.add)
            if single:
                nc.sync.dma_start(out=ov[:, 1, i // 2, i % 2, n * NT:(n + 1) * NT], in_=o[:, cs])
            elif n in (1, 2):
                nc.sync.dma_start(out=ov[:, 1, i // 2, i % 2, 2 * hf * NT:2 * (hf + 1) * NT], in_=o[:])

        def w2_prep():
            w2g = const.tile([P, 4096], BF16, align_bytes=64, tag="wg", name="w2g")
            w2g32 = w2g[:].bitcast(F32).rearrange("q (i g m u) -> q i g m u", g=2, i=4, m=P, u=2)
            for i in range(4):
                wt = psb.tile([P, 4, P], F32, tag="m2", name="wt2")
                wsrc = w2raw[:, i, :].bitcast(F32)
                for r in range(4):
                    nc.tensor.transpose(wt[:, r, :], wsrc[:, P * r:P * r + P], ident[:])
                evac(nc, "SVSV"[i], w2g32[:, i, :, :, :], wt[:].rearrange("q (g u) m -> q g m u", g=2))
            for ip in range(2):
                nc.vector.quantize_mx(out=w2c[:, 2 * ip:2 * ip + 2, :, :].rearrange("q i g m -> q (i g m)").bitcast(FP8X4),
                                      scales=w2s[:, 2 * ip:2 * ip + 2, :, :].rearrange("q i g m -> q (i g m)"),
                                      in_=w2g[:, 2048 * ip:2048 * ip + 2048])

        w1g = const.tile([P, 4096], BF16, align_bytes=64, tag="wg", name="w1g")
        w1g32 = w1g[:].bitcast(F32).rearrange("q (j m u) -> q j m u", j=8, m=P, u=2)
        prw = const.tile([P, 16], F32)
        prm = const.tile([P, 20], F32)
        gw = const.tile([P, 4], F32)
        x_regroup(0)
        x_quant(0)
        for jp in range(4):
            wt = psa.tile([P, 2, 2, P], F32, tag="p1", name="wt1")
            for jj in range(2):
                wsrc = w1raw[:, 2 * jp + jj, :].bitcast(F32)
                for u in range(2):
                    nc.tensor.transpose(wt[:, jj, u, :], wsrc[:, P * u:P * u + P], ident[:])
            nc.scalar.copy(out=w1g32[:, 2 * jp:2 * jp + 2, :, :], in_=wt[:].rearrange("q j u m -> q j m u"))
            j0 = 256 * jp
            nc.vector.quantize_mx(out=w1c[:, j0:j0 + 256].bitcast(FP8X4), scales=w1s[:, j0:j0 + 256],
                                  in_=w1g[:, 4 * j0:4 * j0 + 1024])
            if jp == 0:
                pt = psb.tile([P, P], F32, tag="m2", name="pt")
                nc.tensor.transpose(pt[:], vecs[:].bitcast(F32), ident[:])
                nc.scalar.copy(out=prw[:, 0:10], in_=pt[:, 0:10])
                nc.scalar.copy(out=prm[:], in_=prw[:, 0:10].bitcast(BF16))
        nc.gpsimd.tensor_tensor(out=gw[:], in0=prm[:, 12:16], in1=prm[:, 16:20], op=ALU.mult)

        pieces = [(i, hf) for i in range(4) for hf in range(2)]
        v_todo = [c for c in pieces if c not in PE_FINALS]
        p_todo = [(i, hf, e) for i, hf in PE_FINALS for e in range(2)]
        for w in range(2 - LXR, HALVES + LM2 + 2):
            k = w - LHR
            if 0 <= w < HALVES:
                mm1_gelu(w)
            if 0 <= k < HALVES and k in H_SCALAR:
                h_regroup(k)
            if w == HALVES:
                nc.scalar.activation(out=warm[:], in_=zero1[:], func=ACT.Sqrt)
            if w == LW2:
                w2_prep()
            for q in range(TILES):
                if w == 2 * q + 1 + LM2:
                    for i in range(4):
                        mm2_first(q, i)
            for q in range(1, TILES):
                if 2 * q - LXQ == w:
                    x_quant(q)
            if 0 <= k < HALVES and k not in H_SCALAR:
                h_regroup(k)
            for q in range(1, TILES):
                if 2 * q - LXR == w and q not in X_POOL:
                    x_regroup(q)
            for q in X_POOL:
                if w == 2 * (q - 4) + 1 + LBN[0]:
                    x_regroup_pool(q)
            if 0 <= w - LHQ < HALVES:
                h_quant(w - LHQ)
            for q in range(TILES):
                if w == 2 * q + 1 + LBN[q // 4]:
                    if q == 4:
                        factors1()
                    for i in range(4):
                        stats(q, i)
                    if q + 4 in X_POOL:
                        regroup(nc, "V", st[("xg", q + 4)][:, XSPLIT:, :], xs(q + 4)[:, :, XSPLIT:])
                    if q == 7:
                        for i in range(3):
                            evac_last(i)
                        root2()
                        evac_last(3)
            if w >= VF0 and v_todo:
                final1_v(*v_todo.pop(0))
            if w >= PF0 and p_todo:
                final1_p(*p_todo.pop(0))
        factors2()
        for c in v_todo:
            final1_v(*c)
        for c in p_todo:
            final1_p(*c)
        order = [(i, n) for i in range(4) for n in (3, 2, 0, 1)]
        for i, n in order:
            final2(i, n, (i, n) in order[:2] + order[-2:])
